import numpy as np
import ml_dtypes


def mxq(x, axis, fmt="e4m3"):
    dtype, down = {"e4m3": (ml_dtypes.float8_e4m3fn, 7), "e5m2": (ml_dtypes.float8_e5m2, 14)}[fmt]
    v = np.moveaxis(np.asarray(x, np.float32).astype(ml_dtypes.bfloat16).astype(np.float64), axis, -1)
    blocks = v.reshape(v.shape[:-1] + (-1, 32))
    amax = np.abs(blocks).max(-1, keepdims=True)
    byte = np.maximum(np.where(amax > 0, np.frexp(amax)[1] - 1 + 127, 0) - down, 1)
    scale = np.exp2(byte - 127.0)
    codes = (blocks / scale).astype(np.float32).astype(dtype).astype(np.float64)
    return np.moveaxis((codes * scale).reshape(v.shape), -1, axis)


WIDE = False


def mx_kscale(k):
    if not WIDE:
        return np.ones(k)
    levels = np.array([10, -10, 5, -5, 0])
    if k % 512:
        return np.exp2(np.random.permutation(np.resize(levels, k // 32))).repeat(32)
    a = np.empty((k // 512, 16))
    for p in range(k // 512):
        a[p, :8] = np.random.permutation(np.resize(levels, 8))
        for g in range(8):
            far = levels[np.abs(levels - a[p, g]) >= 10]
            a[p, g + 8] = far[np.random.randint(len(far))]
    return np.exp2(a.ravel()).repeat(32)


BF16 = ml_dtypes.bfloat16


def bf(x):
    return np.asarray(x, np.float32).astype(BF16)


def f64(x):
    return np.asarray(x).astype(np.float64)


B, E, D = 256, 2048, 2048


def setup_inputs():
    s = mx_kscale(E)
    ws = 1.0 / np.sqrt(E)
    return {
        "x": bf(np.random.standard_normal((B, E)) * s),
        "state_A": bf(np.random.uniform(0.0, 1.0, (B, D))),
        "state_B": bf(0.5 + np.random.uniform(0.0, 1.0, (B, D))),
        "state_p": bf(np.random.standard_normal((B, D))),
        "state_x": bf(np.random.standard_normal((B, E)) * s),
        "time_decay": bf(0.5 * np.random.standard_normal(D)),
        "time_first": bf(np.log(0.3) + 0.3 * np.random.standard_normal(D)),
        "time_mix_k": bf(np.random.uniform(0.0, 1.0, (1, E))),
        "time_mix_v": bf(np.random.uniform(0.0, 1.0, (1, E))),
        "W_key": bf(np.random.standard_normal((D, E)) * ws / s[None, :]),
        "W_value": bf(np.random.standard_normal((D, E)) * ws / s[None, :]),
    }


def reference(x, state_A, state_B, state_p, state_x, time_decay, time_first, time_mix_k, time_mix_v, W_key, W_value):
    x, state_x = f64(x), f64(state_x)
    state_A, state_B, state_p = f64(state_A), f64(state_B), f64(state_p)
    mk, mv = f64(time_mix_k), f64(time_mix_v)
    xk = x * mk + state_x * (1.0 - mk)
    xv = x * mv + state_x * (1.0 - mv)
    k = mxq(xk, 1, "e4m3") @ mxq(f64(W_key), 1, "e4m3").T
    v = mxq(xv, 1, "e4m3") @ mxq(f64(W_value), 1, "e4m3").T
    ww = f64(time_first) + k
    p = np.maximum(state_p, ww)
    e1 = np.exp(state_p - p)
    e2 = np.exp(ww - p)
    a = e1 * state_A + e2 * v
    b = e1 * state_B + e2
    td = -np.exp(f64(time_decay))
    ww = state_p + td
    p = np.maximum(ww, k)
    e1 = np.exp(ww - p)
    e2 = np.exp(k - p)
    new_A = e1 * state_A + e2 * v
    new_B = e1 * state_B + e2
    return (a, b, new_A, new_B, p)

@@ -1,0 +1,358 @@
+from contextlib import ExitStack
+
+import concourse.mybir as mybir
+from concourse.masks import make_identity
+
+F32 = mybir.dt.float32
+BF16 = mybir.dt.bfloat16
+U32 = mybir.dt.uint32
+U8 = mybir.dt.uint8
+FP8X4 = mybir.dt.float8_e4m3fn_x4
+ALU = mybir.AluOpType
+ACT = mybir.ActivationFunctionType
+
+P = 128
+ROWS = 256
+E = 2048
+D = 2048
+NT = 512
+TILES = D // NT
+FLOPS = 2 * 2 * ROWS * E * D
+
+
+def tile_rwkv_timemix_for_quant_pa_kernel(
+    tc,
+    x,
+    state_A,
+    state_B,
+    state_p,
+    state_x,
+    time_decay,
+    time_first,
+    time_mix_k,
+    time_mix_v,
+    W_key,
+    W_value,
+    out_0,
+    out_1,
+    out_2,
+    out_3,
+    out_4,
+):
+    nc = tc.nc
+    with ExitStack() as ctx:
+        const = ctx.enter_context(tc.tile_pool(name="const", bufs=1))
+        ring = ctx.enter_context(tc.tile_pool(name="ring", bufs=8))
+        grp = ctx.enter_context(tc.tile_pool(name="grp", bufs=3))
+        cod = ctx.enter_context(tc.tile_pool(name="cod", bufs=3))
+        st = ctx.enter_context(tc.tile_pool(name="st", bufs=2))
+        ep = ctx.enter_context(tc.tile_pool(name="ep", bufs=2))
+        tp = ctx.enter_context(tc.psum_pool(name="tp", bufs=4))
+        acc = ctx.enter_context(tc.psum_pool(name="acc", bufs=4))
+        ctx.enter_context(tc.manual_schedule())
+
+        weights = (W_key, W_value)
+        raw_w = {}
+        states = {}
+
+        def load_w(v, j, h):
+            wr = ring.tile([P, 4096], BF16, tag="ring", name="wr")
+            row0 = NT * j + 256 * h
+            nc.sync.dma_start(
+                out=wr[:].rearrange("p (c k) -> p c k", c=2),
+                in_=weights[v][row0 : row0 + 256, :].rearrange("(c p) k -> p c k", p=P),
+            )
+            raw_w[(v, j, h)] = wr
+
+        def load_states(j):
+            tiles = []
+            for src in (state_p, state_A, state_B):
+                t = st.tile([P, 1024], BF16, tag="st%d" % len(tiles), name="st_t")
+                nc.sync.dma_start(
+                    out=t[:].rearrange("p (r d) -> p r d", r=2),
+                    in_=src.rearrange("(r p) d -> p r d", p=P)[:, :, NT * j : NT * (j + 1)],
+                )
+                tiles.append(t)
+            states[j] = tiles
+
+        mkb = const.tile([P, 32], BF16, name="mkb")
+        with nc.allow_non_contiguous_dma(reason="mix coefficients, four neighbouring k to a partition"):
+            nc.scalar.dma_start(
+                out=mkb[:, 0:16].rearrange("p (g t) -> p g t", t=4),
+                in_=time_mix_k.rearrange("o (g p t) -> p (o g) t", g=4, p=P, t=4),
+            )
+            nc.scalar.dma_start(
+                out=mkb[:, 16:32].rearrange("p (g t) -> p g t", t=4),
+                in_=time_mix_v.rearrange("o (g p t) -> p (o g) t", g=4, p=P, t=4),
+            )
+        vec_rows = const.tile([P, D], BF16, name="vec_rows")
+        nc.vector.memset(vec_rows[:], 0.0)
+        nc.scalar.dma_start(out=vec_rows[0:1, :], in_=time_first.unsqueeze(0))
+        nc.scalar.dma_start(out=vec_rows[1:2, :], in_=time_decay.unsqueeze(0))
+        x_sb = ring.tile([P, 4096], BF16, tag="ring", name="x_sb")
+        sx_sb = ring.tile([P, 4096], BF16, tag="ring", name="sx_sb")
+        for g in range(4):
+            for dst, src in ((sx_sb, state_x), (x_sb, x)):
+                nc.sync.dma_start(
+                    out=dst[:, 1024 * g : 1024 * (g + 1)].rearrange("p (r k) -> p r k", r=2),
+                    in_=src.rearrange("(r p) k -> p r k", p=P)[:, :, 512 * g : 512 * (g + 1)],
+                )
+        for v in range(2):
+            for h in range(2):
+                load_w(v, 0, h)
+        load_states(0)
+        load_w(0, 1, 0)
+        load_w(0, 1, 1)
+
+        ident = const.tile([P, P], F32, name="ident")
+        make_identity(nc, ident[:])
+        identb = const.tile([P, P], BF16, name="identb")
+        make_identity(nc, identb[:])
+        nidentb = const.tile([P, P], BF16, name="nidentb")
+        nc.vector.tensor_scalar_mul(out=nidentb[:], in0=identb[:], scalar1=-1.0)
+        warm_in = const.tile([P, 1], F32, name="warm_in")
+        warm_out = const.tile([P, 1], F32, name="warm_out")
+        nc.vector.memset(warm_in[:], 0.0)
+        nc.scalar.activation(out=warm_out[:], in_=warm_in[:], func=ACT.Exp)
+        mkf = const.tile([P, 32], F32, name="mkf")
+        nc.vector.tensor_copy(out=mkf[:], in_=mkb[:])
+
+        xg = grp.tile([P, 8192], BF16, tag="grp", name="xg", align_bytes=64)
+        sw = sx_sb[:].bitcast(F32)
+        for g in range(4):
+            sb = tp.tile([P, 512], F32, tag="tp", name="sb")
+            for u in range(2):
+                for r in range(2):
+                    src = 512 * g + 256 * r
+                    col = 256 * u + 128 * r
+                    nc.tensor.transpose(sb[:, col : col + 128], sw[:, src + u : src + 256 : 2], ident[:])
+            sxs = ep.tile([P, 1024], BF16, tag="ndd", name="sxs")
+            nc.scalar.copy(out=sxs[:].bitcast(F32), in_=sb[:])
+            plns = [ep.tile([P, 1024], BF16, tag="t%d" % (v + 1), name="pln") for v in range(2)]
+            for u in range(2):
+                dxb = acc.tile([P, 512], F32, tag="acc", name="dxb")
+                for e in range(2):
+                    for r in range(2):
+                        base = 1024 * g + 512 * r
+                        col = 256 * e + 128 * r
+                        xs = x_sb[:, base : base + 512].rearrange("p (w t) -> p w t", t=4)[:, :, 2 * u + e]
+                        ss = sx_sb[:, base : base + 512].rearrange("p (w t) -> p w t", t=4)[:, :, 2 * u + e]
+                        nc.tensor.matmul(out=dxb[:, col : col + 128], lhsT=xs, rhs=identb[:], start=True, stop=False)
+                        nc.tensor.matmul(out=dxb[:, col : col + 128], lhsT=ss, rhs=nidentb[:], start=False, stop=True)
+                for e in range(2):
+                    t = 2 * u + e
+                    sx_pl = sxs[:, 512 * u : 512 * (u + 1)].rearrange("p (n e) -> p n e", e=2)[:, :, e]
+                    for v in range(2):
+                        i = 16 * v + 4 * g + t
+                        nc.vector.scalar_tensor_tensor(
+                            out=plns[v][:, 256 * t : 256 * (t + 1)],
+                            in0=dxb[:, 256 * e : 256 * (e + 1)],
+                            scalar=mkf[:, i : i + 1],
+                            in1=sx_pl,
+                            op0=ALU.mult,
+                            op1=ALU.add,
+                        )
+            for v in range(2):
+                o0 = 4096 * v + 1024 * g
+                nc.gpsimd.tensor_scalar(
+                    out=xg[:, o0 : o0 + 1024].rearrange("p (n t) -> p n t", t=4),
+                    in0=plns[v][:].rearrange("p (t n) -> p n t", t=4),
+                    scalar1=1.0,
+                    scalar2=0.0,
+                    op0=ALU.mult,
+                    op1=ALU.add,
+                )
+        load_w(1, 1, 0)
+        load_w(1, 1, 1)
+
+        xcodes = const.tile([P, 2048], U32, name="xcodes", align_bytes=64)
+        xscl = const.tile([P, 2048], U8, name="xscl", align_bytes=64)
+
+        def quantise_x(v):
+            nc.vector.quantize_mx(
+                out=xcodes[:, 1024 * v : 1024 * (v + 1)].bitcast(FP8X4),
+                scales=xscl[:, 1024 * v : 1024 * (v + 1)],
+                in_=xg[:, 4096 * v : 4096 * (v + 1)],
+            )
+
+        def regroup_w(v, j):
+            gt = grp.tile([P, 8192], BF16, tag="grp", name="gt", align_bytes=64)
+            gw = gt[:].bitcast(F32).rearrange("p (g d u) -> p g d u", g=4, d=NT, u=2)
+            for c in range(4):
+                wf = raw_w[(v, j, c // 2)][:].bitcast(F32)
+                base = 1024 * (c % 2)
+                for hb in range(2):
+                    bank = tp.tile([P, 512], F32, tag="tp", name="bank")
+                    for gi in range(2):
+                        for u in range(2):
+                            src = base + 256 * (2 * hb + gi)
+                            col = 128 * (2 * gi + u)
+                            nc.tensor.transpose(bank[:, col : col + 128], wf[:, src + u : src + 256 : 2], ident[:])
+                    nc.scalar.copy(
+                        out=gw[:, 2 * hb : 2 * hb + 2, 128 * c : 128 * (c + 1), :],
+                        in_=bank[:].rearrange("p (g u d) -> p g d u", g=2, u=2, d=128),
+                    )
+            return gt
+
+        def quantise_w(gt):
+            codes = cod.tile([P, 2048], U32, tag="codes", name="codes", align_bytes=64)
+            scl = cod.tile([P, 2048], U8, tag="scl", name="scl", align_bytes=64)
+            for hb in range(2):
+                nc.vector.quantize_mx(
+                    out=codes[:, 1024 * hb : 1024 * (hb + 1)].bitcast(FP8X4),
+                    scales=scl[:, 1024 * hb : 1024 * (hb + 1)],
+                    in_=gt[:, 4096 * hb : 4096 * (hb + 1)],
+                )
+            return codes, scl
+
+        def project(v, wq, r):
+            codes, scl = wq
+            ps = acc.tile([P, NT], F32, tag="acc", name="ps")
+            for g in range(4):
+                c0 = 1024 * v + 256 * g + 128 * r
+                nc.tensor.matmul_mx(
+                    out=ps[:],
+                    lhsT=xcodes[:, c0 : c0 + 128].bitcast(FP8X4),
+                    lhsT_scale=xscl[:, c0 : c0 + 128],
+                    rhs=codes[:, NT * g : NT * (g + 1)].bitcast(FP8X4),
+                    rhs_scale=scl[:, NT * g : NT * (g + 1)],
+                    start=(g == 0),
+                    stop=(g == 3),
+                )
+            return ps
+
+        tfw = const.tile([P, 4096], F32, name="tfw")
+        tfw_v = tfw[:].rearrange("p (h d) -> p h d", h=2)
+
+        def spread_vectors(j):
+            cols = slice(NT * j, NT * (j + 1))
+            spread = []
+            for row in range(2):
+                ps = tp.tile([P, NT], F32, tag="tp", name="spread_ps")
+                nc.tensor.matmul(
+                    out=ps[:],
+                    lhsT=identb[:, row : row + 1].to_broadcast([P, P]),
+                    rhs=vec_rows[:, cols],
+                    start=True,
+                    stop=True,
+                )
+                spread.append(ps)
+            nc.scalar.copy(out=tfw[:, NT * j : NT * (j + 1)], in_=spread[0][:])
+            nc.scalar.activation(out=tfw[:, D + NT * j : D + NT * (j + 1)], in_=spread[1][:], func=ACT.Exp)
+
+        two = "p (h d) -> p h d"
+
+        def store(dst, j, r, src):
+            nc.sync.dma_start(out=dst[P * r : P * (r + 1), NT * j : NT * (j + 1)], in_=src)
+
+        def per_row_tile(t, r):
+            return t[:, NT * r : NT * (r + 1)]
+
+        def twice(ap):
+            return ap.unsqueeze(1).to_broadcast([P, 2, NT])
+
+        def exponents(j, k_ps):
+            sp_t = states[j][0]
+            nq = [ep.tile([P, NT], F32, tag="nq", name="nq") for r in range(2)]
+            ndd = [ep.tile([P, 1024], F32, tag="ndd", name="ndd") for r in range(2)]
+            xf1 = [ep.tile([P, 1024], F32, tag="xf0", name="xf1") for r in range(2)]
+            xf2 = [ep.tile([P, 1024], F32, tag="xf1", name="xf2") for r in range(2)]
+            p2 = [ep.tile([P, NT], F32, tag="p2", name="p2") for r in range(2)]
+            for r in range(2):
+                nc.vector.tensor_tensor(out=nq[r][:], in0=per_row_tile(sp_t, r), in1=k_ps[r][:], op=ALU.subtract)
+            for r in range(2):
+                nc.vector.tensor_tensor(
+                    out=ndd[r][:].rearrange(two, h=2),
+                    in0=twice(nq[r][:]),
+                    in1=tfw_v[:, :, NT * j : NT * (j + 1)],
+                    op=ALU.subtract,
+                )
+            for r in range(2):
+                nc.scalar.activation(out=xf1[r][:], in_=ndd[r][:], func=ACT.Exp)
+            for r in range(2):
+                nc.scalar.activation(out=xf2[r][:], in_=ndd[r][:], func=ACT.Exp, scale=-1.0)
+            for r in range(2):
+                nc.vector.scalar_tensor_tensor(
+                    out=p2[r][:], in0=ndd[r][:, NT : 2 * NT], scalar=0.0, in1=k_ps[r][:], op0=ALU.max, op1=ALU.add
+                )
+                store(out_4, j, r, p2[r][:])
+            return xf1, xf2
+
+        def numerators(j, v_ps, xf1, xf2):
+            a_t = states[j][1]
+            t1 = [ep.tile([P, 1024], F32, tag="t1", name="t1") for r in range(2)]
+            t2 = [ep.tile([P, 1024], F32, tag="t2", name="t2") for r in range(2)]
+            for r in range(2):
+                nc.vector.scalar_tensor_tensor(
+                    out=t1[r][:].rearrange(two, h=2),
+                    in0=xf1[r][:].rearrange(two, h=2),
+                    scalar=1.0,
+                    in1=twice(per_row_tile(a_t, r)),
+                    op0=ALU.min,
+                    op1=ALU.mult,
+                )
+            for r in range(2):
+                nc.vector.scalar_tensor_tensor(
+                    out=t2[r][:].rearrange(two, h=2),
+                    in0=xf2[r][:].rearrange(two, h=2),
+                    scalar=1.0,
+                    in1=twice(v_ps[r][:]),
+                    op0=ALU.min,
+                    op1=ALU.mult,
+                )
+            for r in range(2):
+                nc.vector.tensor_tensor(out=t1[r][:], in0=t1[r][:], in1=t2[r][:], op=ALU.add)
+                store(out_0, j, r, t1[r][:, 0:NT])
+                store(out_2, j, r, t1[r][:, NT : 2 * NT])
+
+        def denominators(j, xf1, xf2):
+            b_t = states[j][2]
+            for r in range(2):
+                nc.vector.scalar_tensor_tensor(
+                    out=xf1[r][:].rearrange(two, h=2),
+                    in0=xf1[r][:].rearrange(two, h=2),
+                    scalar=1.0,
+                    in1=twice(per_row_tile(b_t, r)),
+                    op0=ALU.min,
+                    op1=ALU.mult,
+                )
+            for r in range(2):
+                nc.vector.scalar_tensor_tensor(
+                    out=xf2[r][:], in0=xf2[r][:], scalar=1.0, in1=xf1[r][:], op0=ALU.min, op1=ALU.add
+                )
+                store(out_1, j, r, xf2[r][:, 0:NT])
+                store(out_3, j, r, xf2[r][:, NT : 2 * NT])
+
+        gt_k = regroup_w(0, 0)
+        load_states(1)
+        spread_vectors(0)
+        wq_k = quantise_w(gt_k)
+        quantise_x(0)
+        gt_v = regroup_w(1, 0)
+        wq_v = quantise_w(gt_v)
+        quantise_x(1)
+        k_ps = [project(0, wq_k, r) for r in range(2)]
+        v_ps = [project(1, wq_v, r) for r in range(2)]
+
+        for j in range(TILES):
+            xf1, xf2 = exponents(j, k_ps)
+            if j + 1 < TILES:
+                spread_vectors(j + 1)
+            if j + 2 < TILES:
+                load_w(0, j + 2, 0)
+                load_w(0, j + 2, 1)
+            if j + 1 < TILES:
+                gt_k = regroup_w(0, j + 1)
+                gt_v = regroup_w(1, j + 1)
+            numerators(j, v_ps, xf1, xf2)
+            if j + 2 < TILES:
+                load_w(1, j + 2, 0)
+                load_w(1, j + 2, 1)
+            denominators(j, xf1, xf2)
+            if j + 2 < TILES:
+                load_states(j + 2)
+            if j + 1 < TILES:
+                wq_k = quantise_w(gt_k)
+                wq_v = quantise_w(gt_v)
+                k_ps = [project(0, wq_k, r) for r in range(2)]
+                v_ps = [project(1, wq_v, r) for r in range(2)]

@@ -44,9 +44,10 @@ def tile_rwkv_timemix_for_quant_pa_kernel(
         const = ctx.enter_context(tc.tile_pool(name="const", bufs=1))
         ring = ctx.enter_context(tc.tile_pool(name="ring", bufs=8))
         grp = ctx.enter_context(tc.tile_pool(name="grp", bufs=3))
-        cod = ctx.enter_context(tc.tile_pool(name="cod", bufs=3))
+        cod = ctx.enter_context(tc.tile_pool(name="cod", bufs=2))
         st = ctx.enter_context(tc.tile_pool(name="st", bufs=2))
         ep = ctx.enter_context(tc.tile_pool(name="ep", bufs=2))
+        hp = ctx.enter_context(tc.tile_pool(name="hp", bufs=4))
         tp = ctx.enter_context(tc.psum_pool(name="tp", bufs=4))
         acc = ctx.enter_context(tc.psum_pool(name="acc", bufs=4))
         ctx.enter_context(tc.manual_schedule())
@@ -75,6 +76,9 @@ def tile_rwkv_timemix_for_quant_pa_kernel(
                 tiles.append(t)
             states[j] = tiles
 
+        warm_in = const.tile([P, 1], F32, name="warm_in")
+        warm_out = const.tile([P, 1], F32, name="warm_out")
+        nc.vector.memset(warm_in[:], 0.0)
         mkb = const.tile([P, 32], BF16, name="mkb")
         with nc.allow_non_contiguous_dma(reason="mix coefficients, four neighbouring k to a partition"):
             nc.scalar.dma_start(
@@ -89,6 +93,7 @@ def tile_rwkv_timemix_for_quant_pa_kernel(
         nc.vector.memset(vec_rows[:], 0.0)
         nc.scalar.dma_start(out=vec_rows[0:1, :], in_=time_first.unsqueeze(0))
         nc.scalar.dma_start(out=vec_rows[1:2, :], in_=time_decay.unsqueeze(0))
+        nc.scalar.activation(out=warm_out[:], in_=warm_in[:], func=ACT.Exp)
         x_sb = ring.tile([P, 4096], BF16, tag="ring", name="x_sb")
         sx_sb = ring.tile([P, 4096], BF16, tag="ring", name="sx_sb")
         for g in range(4):
@@ -110,58 +115,72 @@ def tile_rwkv_timemix_for_quant_pa_kernel(
         make_identity(nc, identb[:])
         nidentb = const.tile([P, P], BF16, name="nidentb")
         nc.vector.tensor_scalar_mul(out=nidentb[:], in0=identb[:], scalar1=-1.0)
-        warm_in = const.tile([P, 1], F32, name="warm_in")
-        warm_out = const.tile([P, 1], F32, name="warm_out")
-        nc.vector.memset(warm_in[:], 0.0)
-        nc.scalar.activation(out=warm_out[:], in_=warm_in[:], func=ACT.Exp)
         mkf = const.tile([P, 32], F32, name="mkf")
         nc.vector.tensor_copy(out=mkf[:], in_=mkb[:])
 
+        omk = const.tile([P, 32], F32, name="omk")
+        nc.vector.tensor_scalar(out=omk[:], in0=mkf[:], scalar1=-1.0, scalar2=1.0, op0=ALU.mult, op1=ALU.add)
+
         xg = grp.tile([P, 8192], BF16, tag="grp", name="xg", align_bytes=64)
         sw = sx_sb[:].bitcast(F32)
-        for g in range(4):
-            sb = tp.tile([P, 512], F32, tag="tp", name="sb")
+        xw = x_sb[:].bitcast(F32)
+        xbank = []
+
+        def of_t(bank, t):
+            half = bank[:, 512 * (t // 2) : 512 * (t // 2 + 1)]
+            return half.rearrange("p (n e) -> p n e", e=2)[:, :, t % 2]
+
+        def transpose_group(words, g, bank):
             for u in range(2):
                 for r in range(2):
                     src = 512 * g + 256 * r
                     col = 256 * u + 128 * r
-                    nc.tensor.transpose(sb[:, col : col + 128], sw[:, src + u : src + 256 : 2], ident[:])
-            sxs = ep.tile([P, 1024], BF16, tag="ndd", name="sxs")
-            nc.scalar.copy(out=sxs[:].bitcast(F32), in_=sb[:])
-            plns = [ep.tile([P, 1024], BF16, tag="t%d" % (v + 1), name="pln") for v in range(2)]
-            for u in range(2):
-                dxb = acc.tile([P, 512], F32, tag="acc", name="dxb")
-                for e in range(2):
-                    for r in range(2):
-                        base = 1024 * g + 512 * r
-                        col = 256 * e + 128 * r
-                        xs = x_sb[:, base : base + 512].rearrange("p (w t) -> p w t", t=4)[:, :, 2 * u + e]
-                        ss = sx_sb[:, base : base + 512].rearrange("p (w t) -> p w t", t=4)[:, :, 2 * u + e]
-                        nc.tensor.matmul(out=dxb[:, col : col + 128], lhsT=xs, rhs=identb[:], start=True, stop=False)
-                        nc.tensor.matmul(out=dxb[:, col : col + 128], lhsT=ss, rhs=nidentb[:], start=False, stop=True)
-                for e in range(2):
-                    t = 2 * u + e
-                    sx_pl = sxs[:, 512 * u : 512 * (u + 1)].rearrange("p (n e) -> p n e", e=2)[:, :, e]
-                    for v in range(2):
-                        i = 16 * v + 4 * g + t
-                        nc.vector.scalar_tensor_tensor(
-                            out=plns[v][:, 256 * t : 256 * (t + 1)],
-                            in0=dxb[:, 256 * e : 256 * (e + 1)],
-                            scalar=mkf[:, i : i + 1],
-                            in1=sx_pl,
-                            op0=ALU.mult,
-                            op1=ALU.add,
-                        )
-            for v in range(2):
-                o0 = 4096 * v + 1024 * g
-                nc.gpsimd.tensor_scalar(
-                    out=xg[:, o0 : o0 + 1024].rearrange("p (n t) -> p n t", t=4),
-                    in0=plns[v][:].rearrange("p (t n) -> p n t", t=4),
-                    scalar1=1.0,
-                    scalar2=0.0,
+                    nc.tensor.transpose(bank[:, col : col + 128], words[:, src + u : src + 256 : 2], ident[:])
+
+        def scaled_sx(v, g, bank):
+            y = ep.tile([P, 1024], F32, tag=("t1", "t2")[v], name="y")
+            for t in range(4):
+                i = 16 * v + 4 * g + t
+                nc.scalar.activation(
+                    out=y[:, 256 * t : 256 * (t + 1)],
+                    in_=of_t(bank[:].bitcast(BF16), t),
+                    func=ACT.Copy,
+                    scale=omk[:, i : i + 1],
+                )
+            return y
+
+        def mix(v, g, y):
+            pln = hp.tile([P, 1024], BF16, tag="hp", name="pln")
+            for t in range(4):
+                i = 16 * v + 4 * g + t
+                nc.vector.scalar_tensor_tensor(
+                    out=pln[:, 256 * t : 256 * (t + 1)],
+                    in0=of_t(xbank[g][:].bitcast(BF16), t),
+                    scalar=mkf[:, i : i + 1],
+                    in1=y[:, 256 * t : 256 * (t + 1)],
                     op0=ALU.mult,
                     op1=ALU.add,
                 )
+            o0 = 4096 * v + 1024 * g
+            nc.gpsimd.tensor_scalar(
+                out=xg[:, o0 : o0 + 1024].rearrange("p (n t) -> p n t", t=4),
+                in0=pln[:].rearrange("p (t n) -> p n t", t=4),
+                scalar1=1.0,
+                scalar2=0.0,
+                op0=ALU.mult,
+                op1=ALU.add,
+            )
+
+        sbank = []
+        for g in range(4):
+            sb = tp.tile([P, 512], F32, tag="tp", name="sb")
+            transpose_group(sw, g, sb)
+            sbank.append(sb)
+            xb = acc.tile([P, 512], F32, tag="acc", name="xb")
+            transpose_group(xw, g, xb)
+            xbank.append(xb)
+        for v, g in ((0, 0), (0, 1), (1, 0), (0, 2), (1, 1), (0, 3), (1, 2), (1, 3)):
+            mix(v, g, scaled_sx(v, g, sbank[g]))
         load_w(1, 1, 0)
         load_w(1, 1, 1)
 
@@ -175,13 +194,15 @@ def tile_rwkv_timemix_for_quant_pa_kernel(
                 in_=xg[:, 4096 * v : 4096 * (v + 1)],
             )
 
-        def regroup_w(v, j):
-            gt = grp.tile([P, 8192], BF16, tag="grp", name="gt", align_bytes=64)
+        def new_gt():
+            return grp.tile([P, 8192], BF16, tag="grp", name="gt", align_bytes=64)
+
+        def regroup_w(v, j, gt, halves=(0, 1)):
             gw = gt[:].bitcast(F32).rearrange("p (g d u) -> p g d u", g=4, d=NT, u=2)
-            for c in range(4):
-                wf = raw_w[(v, j, c // 2)][:].bitcast(F32)
-                base = 1024 * (c % 2)
-                for hb in range(2):
+            for hb in halves:
+                for c in range(4):
+                    wf = raw_w[(v, j, c // 2)][:].bitcast(F32)
+                    base = 1024 * (c % 2)
                     bank = tp.tile([P, 512], F32, tag="tp", name="bank")
                     for gi in range(2):
                         for u in range(2):
@@ -192,18 +213,20 @@ def tile_rwkv_timemix_for_quant_pa_kernel(
                         out=gw[:, 2 * hb : 2 * hb + 2, 128 * c : 128 * (c + 1), :],
                         in_=bank[:].rearrange("p (g u d) -> p g d u", g=2, u=2, d=128),
                     )
-            return gt
 
-        def quantise_w(gt):
+        def new_codes():
             codes = cod.tile([P, 2048], U32, tag="codes", name="codes", align_bytes=64)
             scl = cod.tile([P, 2048], U8, tag="scl", name="scl", align_bytes=64)
-            for hb in range(2):
+            return codes, scl
+
+        def quantise_w(gt, wq, halves=(0, 1)):
+            codes, scl = wq
+            for hb in halves:
                 nc.vector.quantize_mx(
                     out=codes[:, 1024 * hb : 1024 * (hb + 1)].bitcast(FP8X4),
                     scales=scl[:, 1024 * hb : 1024 * (hb + 1)],
                     in_=gt[:, 4096 * hb : 4096 * (hb + 1)],
                 )
-            return codes, scl
 
         def project(v, wq, r):
             codes, scl = wq
@@ -221,24 +244,49 @@ def tile_rwkv_timemix_for_quant_pa_kernel(
                 )
             return ps
 
-        tfw = const.tile([P, 4096], F32, name="tfw")
-        tfw_v = tfw[:].rearrange("p (h d) -> p h d", h=2)
+        delta = const.tile([P, D], F32, name="delta")
+        h_tiles = {}
+        spread = {}
+
+        def row_spread(j, row, name):
+            ps = tp.tile([P, NT], F32, tag="tp", name=name)
+            nc.tensor.matmul(
+                out=ps[:],
+                lhsT=identb[:, row : row + 1].to_broadcast([P, P]),
+                rhs=vec_rows[:, NT * j : NT * (j + 1)],
+                start=True,
+                stop=True,
+            )
+            return ps
 
         def spread_vectors(j):
-            cols = slice(NT * j, NT * (j + 1))
-            spread = []
-            for row in range(2):
-                ps = tp.tile([P, NT], F32, tag="tp", name="spread_ps")
+            tf_ps = row_spread(j, 0, "tf_ps")
+            td_ps = row_spread(j, 1, "td_ps")
+            etd = ep.tile([P, NT], F32, tag="etd", name="etd")
+            nc.scalar.activation(out=etd[:], in_=td_ps[:], func=ACT.Exp)
+            spread[j] = (tf_ps, etd)
+
+        def make_delta(j):
+            tf_ps, etd = spread[j]
+            nc.vector.tensor_tensor(out=delta[:, NT * j : NT * (j + 1)], in0=tf_ps[:], in1=etd[:], op=ALU.subtract)
+
+        def make_h(j):
+            h_tiles[j] = []
+            for r in range(2):
+                ps = tp.tile([P, NT], F32, tag="tp", name="h_ps")
+                nc.tensor.matmul(
+                    out=ps[:], lhsT=identb[:], rhs=states[j][0][:, NT * r : NT * (r + 1)], start=True, stop=False
+                )
                 nc.tensor.matmul(
                     out=ps[:],
-                    lhsT=identb[:, row : row + 1].to_broadcast([P, P]),
-                    rhs=vec_rows[:, cols],
-                    start=True,
+                    lhsT=nidentb[:, 0:1].to_broadcast([P, P]),
+                    rhs=vec_rows[:, NT * j : NT * (j + 1)],
+                    start=False,
                     stop=True,
                 )
-                spread.append(ps)
-            nc.scalar.copy(out=tfw[:, NT * j : NT * (j + 1)], in_=spread[0][:])
-            nc.scalar.activation(out=tfw[:, D + NT * j : D + NT * (j + 1)], in_=spread[1][:], func=ACT.Exp)
+                h = hp.tile([P, NT], F32, tag="h", name="h")
+                nc.scalar.copy(out=h[:], in_=ps[:])
+                h_tiles[j].append(h)
 
         two = "p (h d) -> p h d"
 
@@ -252,20 +300,18 @@ def tile_rwkv_timemix_for_quant_pa_kernel(
             return ap.unsqueeze(1).to_broadcast([P, 2, NT])
 
         def exponents(j, k_ps):
-            sp_t = states[j][0]
-            nq = [ep.tile([P, NT], F32, tag="nq", name="nq") for r in range(2)]
             ndd = [ep.tile([P, 1024], F32, tag="ndd", name="ndd") for r in range(2)]
             xf1 = [ep.tile([P, 1024], F32, tag="xf0", name="xf1") for r in range(2)]
             xf2 = [ep.tile([P, 1024], F32, tag="xf1", name="xf2") for r in range(2)]
             p2 = [ep.tile([P, NT], F32, tag="p2", name="p2") for r in range(2)]
             for r in range(2):
-                nc.vector.tensor_tensor(out=nq[r][:], in0=per_row_tile(sp_t, r), in1=k_ps[r][:], op=ALU.subtract)
+                nc.vector.tensor_tensor(out=ndd[r][:, 0:NT], in0=h_tiles[j][r][:], in1=k_ps[r][:], op=ALU.subtract)
             for r in range(2):
                 nc.vector.tensor_tensor(
-                    out=ndd[r][:].rearrange(two, h=2),
-                    in0=twice(nq[r][:]),
-                    in1=tfw_v[:, :, NT * j : NT * (j + 1)],
-                    op=ALU.subtract,
+                    out=ndd[r][:, NT : 2 * NT],
+                    in0=ndd[r][:, 0:NT],
+                    in1=delta[:, NT * j : NT * (j + 1)],
+                    op=ALU.add,
                 )
             for r in range(2):
                 nc.scalar.activation(out=xf1[r][:], in_=ndd[r][:], func=ACT.Exp)
@@ -278,10 +324,9 @@ def tile_rwkv_timemix_for_quant_pa_kernel(
                 store(out_4, j, r, p2[r][:])
             return xf1, xf2
 
-        def numerators(j, v_ps, xf1, xf2):
-            a_t = states[j][1]
+        def state_terms(j, xf1):
+            a_t, b_t = states[j][1], states[j][2]
             t1 = [ep.tile([P, 1024], F32, tag="t1", name="t1") for r in range(2)]
-            t2 = [ep.tile([P, 1024], F32, tag="t2", name="t2") for r in range(2)]
             for r in range(2):
                 nc.vector.scalar_tensor_tensor(
                     out=t1[r][:].rearrange(two, h=2),
@@ -293,22 +338,6 @@ def tile_rwkv_timemix_for_quant_pa_kernel(
                 )
             for r in range(2):
                 nc.vector.scalar_tensor_tensor(
-                    out=t2[r][:].rearrange(two, h=2),
-                    in0=xf2[r][:].rearrange(two, h=2),
-                    scalar=1.0,
-                    in1=twice(v_ps[r][:]),
-                    op0=ALU.min,
-                    op1=ALU.mult,
-                )
-            for r in range(2):
-                nc.vector.tensor_tensor(out=t1[r][:], in0=t1[r][:], in1=t2[r][:], op=ALU.add)
-                store(out_0, j, r, t1[r][:, 0:NT])
-                store(out_2, j, r, t1[r][:, NT : 2 * NT])
-
-        def denominators(j, xf1, xf2):
-            b_t = states[j][2]
-            for r in range(2):
-                nc.vector.scalar_tensor_tensor(
                     out=xf1[r][:].rearrange(two, h=2),
                     in0=xf1[r][:].rearrange(two, h=2),
                     scalar=1.0,
@@ -316,6 +345,22 @@ def tile_rwkv_timemix_for_quant_pa_kernel(
                     op0=ALU.min,
                     op1=ALU.mult,
                 )
+            return t1
+
+        def value_terms(j, v_ps, xf2):
+            t2 = [ep.tile([P, 1024], F32, tag="t2", name="t2") for r in range(2)]
+            for r in range(2):
+                nc.vector.scalar_tensor_tensor(
+                    out=t2[r][:].rearrange(two, h=2),
+                    in0=xf2[r][:].rearrange(two, h=2),
+                    scalar=1.0,
+                    in1=twice(v_ps[r][:]),
+                    op0=ALU.min,
+                    op1=ALU.mult,
+                )
+            return t2
+
+        def denominators(j, xf1, xf2):
             for r in range(2):
                 nc.vector.scalar_tensor_tensor(
                     out=xf2[r][:], in0=xf2[r][:], scalar=1.0, in1=xf1[r][:], op0=ALU.min, op1=ALU.add
@@ -323,36 +368,55 @@ def tile_rwkv_timemix_for_quant_pa_kernel(
                 store(out_1, j, r, xf2[r][:, 0:NT])
                 store(out_3, j, r, xf2[r][:, NT : 2 * NT])
 
-        gt_k = regroup_w(0, 0)
+        def numerators(j, t1, t2):
+            for r in range(2):
+                nc.vector.tensor_tensor(out=t1[r][:], in0=t1[r][:], in1=t2[r][:], op=ALU.add)
+                store(out_0, j, r, t1[r][:, 0:NT])
+                store(out_2, j, r, t1[r][:, NT : 2 * NT])
+
+        gt_k, gt_v = new_gt(), new_gt()
+        wq_k, wq_v = new_codes(), new_codes()
+        regroup_w(0, 0, gt_k)
         load_states(1)
         spread_vectors(0)
-        wq_k = quantise_w(gt_k)
+        make_h(0)
         quantise_x(0)
-        gt_v = regroup_w(1, 0)
-        wq_v = quantise_w(gt_v)
-        quantise_x(1)
+        quantise_w(gt_k, wq_k)
+        make_delta(0)
+        regroup_w(1, 0, gt_v, (0,))
         k_ps = [project(0, wq_k, r) for r in range(2)]
+        regroup_w(1, 0, gt_v, (1,))
+        quantise_x(1)
+        quantise_w(gt_v, wq_v, (0,))
+        xf1, xf2 = exponents(0, k_ps)
+        quantise_w(gt_v, wq_v, (1,))
         v_ps = [project(1, wq_v, r) for r in range(2)]
 
         for j in range(TILES):
-            xf1, xf2 = exponents(j, k_ps)
-            if j + 1 < TILES:
-                spread_vectors(j + 1)
+            if j > 0:
+                xf1, xf2 = exponents(j, k_ps)
             if j + 2 < TILES:
                 load_w(0, j + 2, 0)
                 load_w(0, j + 2, 1)
             if j + 1 < TILES:
-                gt_k = regroup_w(0, j + 1)
-                gt_v = regroup_w(1, j + 1)
-            numerators(j, v_ps, xf1, xf2)
+                gt_k, gt_v = new_gt(), new_gt()
+                regroup_w(0, j + 1, gt_k)
+                spread_vectors(j + 1)
+                make_h(j + 1)
+                regroup_w(1, j + 1, gt_v)
+            t1 = state_terms(j, xf1)
+            t2 = value_terms(j, v_ps, xf2)
+            denominators(j, xf1, xf2)
             if j + 2 < TILES:
                 load_w(1, j + 2, 0)
                 load_w(1, j + 2, 1)
-            denominators(j, xf1, xf2)
+            numerators(j, t1, t2)
             if j + 2 < TILES:
                 load_states(j + 2)
             if j + 1 < TILES:
-                wq_k = quantise_w(gt_k)
-                wq_v = quantise_w(gt_v)
+                wq_k, wq_v = new_codes(), new_codes()
+                quantise_w(gt_k, wq_k)
+                make_delta(j + 1)
+                quantise_w(gt_v, wq_v)
                 k_ps = [project(0, wq_k, r) for r in range(2)]
                 v_ps = [project(1, wq_v, r) for r in range(2)]

@@ -89,11 +89,11 @@ def tile_rwkv_timemix_for_quant_pa_kernel(
                 out=mkb[:, 16:32].rearrange("p (g t) -> p g t", t=4),
                 in_=time_mix_v.rearrange("o (g p t) -> p (o g) t", g=4, p=P, t=4),
             )
+        nc.scalar.activation(out=warm_out[:], in_=warm_in[:], func=ACT.Exp)
         vec_rows = const.tile([P, D], BF16, name="vec_rows")
         nc.vector.memset(vec_rows[:], 0.0)
         nc.scalar.dma_start(out=vec_rows[0:1, :], in_=time_first.unsqueeze(0))
         nc.scalar.dma_start(out=vec_rows[1:2, :], in_=time_decay.unsqueeze(0))
-        nc.scalar.activation(out=warm_out[:], in_=warm_in[:], func=ACT.Exp)
         x_sb = ring.tile([P, 4096], BF16, tag="ring", name="x_sb")
         sx_sb = ring.tile([P, 4096], BF16, tag="ring", name="sx_sb")
         for g in range(4):
@@ -347,32 +347,30 @@ def tile_rwkv_timemix_for_quant_pa_kernel(
                 )
             return t1
 
-        def value_terms(j, v_ps, xf2):
-            t2 = [ep.tile([P, 1024], F32, tag="t2", name="t2") for r in range(2)]
-            for r in range(2):
-                nc.vector.scalar_tensor_tensor(
-                    out=t2[r][:].rearrange(two, h=2),
-                    in0=xf2[r][:].rearrange(two, h=2),
-                    scalar=1.0,
-                    in1=twice(v_ps[r][:]),
-                    op0=ALU.min,
-                    op1=ALU.mult,
-                )
+        def value_term(j, v_ps, xf2, r):
+            t2 = ep.tile([P, 1024], F32, tag="t2", name="t2")
+            nc.vector.scalar_tensor_tensor(
+                out=t2[:].rearrange(two, h=2),
+                in0=xf2[r][:].rearrange(two, h=2),
+                scalar=1.0,
+                in1=twice(v_ps[r][:]),
+                op0=ALU.min,
+                op1=ALU.mult,
+            )
             return t2
 
         def denominators(j, xf1, xf2):
             for r in range(2):
                 nc.vector.scalar_tensor_tensor(
-                    out=xf2[r][:], in0=xf2[r][:], scalar=1.0, in1=xf1[r][:], op0=ALU.min, op1=ALU.add
+                    out=xf1[r][:], in0=xf2[r][:], scalar=1.0, in1=xf1[r][:], op0=ALU.min, op1=ALU.add
                 )
-                store(out_1, j, r, xf2[r][:, 0:NT])
-                store(out_3, j, r, xf2[r][:, NT : 2 * NT])
+                store(out_1, j, r, xf1[r][:, 0:NT])
+                store(out_3, j, r, xf1[r][:, NT : 2 * NT])
 
-        def numerators(j, t1, t2):
-            for r in range(2):
-                nc.vector.tensor_tensor(out=t1[r][:], in0=t1[r][:], in1=t2[r][:], op=ALU.add)
-                store(out_0, j, r, t1[r][:, 0:NT])
-                store(out_2, j, r, t1[r][:, NT : 2 * NT])
+        def numerator(j, r, t1, t2, engine):
+            engine.tensor_tensor(out=t2[:], in0=t1[:], in1=t2[:], op=ALU.add)
+            store(out_0, j, r, t2[:, 0:NT])
+            store(out_2, j, r, t2[:, NT : 2 * NT])
 
         gt_k, gt_v = new_gt(), new_gt()
         wq_k, wq_v = new_codes(), new_codes()
@@ -393,30 +391,37 @@ def tile_rwkv_timemix_for_quant_pa_kernel(
         v_ps = [project(1, wq_v, r) for r in range(2)]
 
         for j in range(TILES):
+            last = j + 1 == TILES
             if j > 0:
                 xf1, xf2 = exponents(j, k_ps)
+                numerator(j - 1, 1, t1[1], t2[1], nc.vector)
             if j + 2 < TILES:
                 load_w(0, j + 2, 0)
                 load_w(0, j + 2, 1)
-            if j + 1 < TILES:
+            if not last:
                 gt_k, gt_v = new_gt(), new_gt()
                 regroup_w(0, j + 1, gt_k)
+                regroup_w(1, j + 1, gt_v)
                 spread_vectors(j + 1)
                 make_h(j + 1)
-                regroup_w(1, j + 1, gt_v)
             t1 = state_terms(j, xf1)
-            t2 = value_terms(j, v_ps, xf2)
             denominators(j, xf1, xf2)
             if j + 2 < TILES:
                 load_w(1, j + 2, 0)
                 load_w(1, j + 2, 1)
-            numerators(j, t1, t2)
-            if j + 2 < TILES:
                 load_states(j + 2)
-            if j + 1 < TILES:
+            if not last:
                 wq_k, wq_v = new_codes(), new_codes()
                 quantise_w(gt_k, wq_k)
-                make_delta(j + 1)
-                quantise_w(gt_v, wq_v)
                 k_ps = [project(0, wq_k, r) for r in range(2)]
+                quantise_w(gt_v, wq_v)
+            t2 = [value_term(j, v_ps, xf2, 0)]
+            if not last:
+                numerator(j, 0, t1[0], t2[0], nc.gpsimd)
+            t2.append(value_term(j, v_ps, xf2, 1))
+            if not last:
+                make_delta(j + 1)
                 v_ps = [project(1, wq_v, r) for r in range(2)]
+            else:
+                for r in range(2):
+                    numerator(j, r, t1[r], t2[r], nc.vector)

@@ -48,8 +48,9 @@ def tile_rwkv_timemix_for_quant_pa_kernel(
         st = ctx.enter_context(tc.tile_pool(name="st", bufs=2))
         ep = ctx.enter_context(tc.tile_pool(name="ep", bufs=2))
         hp = ctx.enter_context(tc.tile_pool(name="hp", bufs=4))
-        tp = ctx.enter_context(tc.psum_pool(name="tp", bufs=4))
-        acc = ctx.enter_context(tc.psum_pool(name="acc", bufs=4))
+        dl = ctx.enter_context(tc.psum_pool(name="dl", bufs=1))
+        tp = ctx.enter_context(tc.psum_pool(name="tp", bufs=3))
+        acc = ctx.enter_context(tc.psum_pool(name="acc", bufs=2))
         ctx.enter_context(tc.manual_schedule())
 
         weights = (W_key, W_value)
@@ -65,16 +66,18 @@ def tile_rwkv_timemix_for_quant_pa_kernel(
             )
             raw_w[(v, j, h)] = wr
 
+        def load_state(j, i):
+            src = (state_p, state_A, state_B)[i]
+            t = st.tile([P, 1024], BF16, tag="st%d" % i, name="st_t")
+            nc.sync.dma_start(
+                out=t[:].rearrange("p (r d) -> p r d", r=2),
+                in_=src.rearrange("(r p) d -> p r d", p=P)[:, :, NT * j : NT * (j + 1)],
+            )
+            states.setdefault(j, []).append(t)
+
         def load_states(j):
-            tiles = []
-            for src in (state_p, state_A, state_B):
-                t = st.tile([P, 1024], BF16, tag="st%d" % len(tiles), name="st_t")
-                nc.sync.dma_start(
-                    out=t[:].rearrange("p (r d) -> p r d", r=2),
-                    in_=src.rearrange("(r p) d -> p r d", p=P)[:, :, NT * j : NT * (j + 1)],
-                )
-                tiles.append(t)
-            states[j] = tiles
+            for i in range(3):
+                load_state(j, i)
 
         warm_in = const.tile([P, 1], F32, name="warm_in")
         warm_out = const.tile([P, 1], F32, name="warm_out")
@@ -90,10 +93,19 @@ def tile_rwkv_timemix_for_quant_pa_kernel(
                 in_=time_mix_v.rearrange("o (g p t) -> p (o g) t", g=4, p=P, t=4),
             )
         nc.scalar.activation(out=warm_out[:], in_=warm_in[:], func=ACT.Exp)
-        vec_rows = const.tile([P, D], BF16, name="vec_rows")
+        td_rows = const.tile([P, NT], BF16, name="td_rows")
+        vec_rows = const.tile([P, NT], BF16, name="vec_rows")
+        nc.vector.memset(td_rows[:], 0.0)
         nc.vector.memset(vec_rows[:], 0.0)
-        nc.scalar.dma_start(out=vec_rows[0:1, :], in_=time_first.unsqueeze(0))
-        nc.scalar.dma_start(out=vec_rows[1:2, :], in_=time_decay.unsqueeze(0))
+        nc.scalar.activation(out=warm_out[:], in_=warm_in[:], func=ACT.Exp)
+        td_rows = const.tile([P, NT], BF16, name="td_rows")
+        vec_rows = const.tile([P, NT], BF16, name="vec_rows")
+        nc.vector.memset(td_rows[:], 0.0)
+        nc.vector.memset(vec_rows[:], 0.0)
+        for row in (0, 64, 96):
+            nc.scalar.dma_start(out=td_rows[row : row + TILES, :], in_=time_decay.rearrange("(j d) -> j d", j=TILES))
+        nc.scalar.dma_start(out=vec_rows[32 : 32 + TILES, :], in_=time_first.rearrange("(j d) -> j d", j=TILES))
+        nc.scalar.activation(out=warm_out[:], in_=warm_in[:], func=ACT.Exp)
         x_sb = ring.tile([P, 4096], BF16, tag="ring", name="x_sb")
         sx_sb = ring.tile([P, 4096], BF16, tag="ring", name="sx_sb")
         for g in range(4):
@@ -102,10 +114,12 @@ def tile_rwkv_timemix_for_quant_pa_kernel(
                     out=dst[:, 1024 * g : 1024 * (g + 1)].rearrange("p (r k) -> p r k", r=2),
                     in_=src.rearrange("(r p) k -> p r k", p=P)[:, :, 512 * g : 512 * (g + 1)],
                 )
+        load_state(0, 0)
         for v in range(2):
             for h in range(2):
                 load_w(v, 0, h)
-        load_states(0)
+        load_state(0, 1)
+        load_state(0, 2)
         load_w(0, 1, 0)
         load_w(0, 1, 1)
 
@@ -114,7 +128,11 @@ def tile_rwkv_timemix_for_quant_pa_kernel(
         identb = const.tile([P, P], BF16, name="identb")
         make_identity(nc, identb[:])
         nidentb = const.tile([P, P], BF16, name="nidentb")
-        nc.vector.tensor_scalar_mul(out=nidentb[:], in0=identb[:], scalar1=-1.0)
+        nc.gpsimd.tensor_scalar(out=nidentb[:], in0=identb[:], scalar1=-1.0, scalar2=0.0, op0=ALU.mult, op1=ALU.add)
+        sel = const.tile([P, TILES], BF16, name="sel")
+        nc.gpsimd.tensor_tensor(out=sel[:], in0=identb[:, 32 : 32 + TILES], in1=identb[:, 0:TILES], op=ALU.subtract)
+        nc.gpsimd.tensor_tensor(out=sel[:], in0=sel[:], in1=identb[:, 64 : 64 + TILES], op=ALU.subtract)
+        nc.gpsimd.tensor_tensor(out=sel[:], in0=sel[:], in1=identb[:, 96 : 96 + TILES], op=ALU.subtract)
         mkf = const.tile([P, 32], F32, name="mkf")
         nc.vector.tensor_copy(out=mkf[:], in_=mkb[:])
 
@@ -138,7 +156,7 @@ def tile_rwkv_timemix_for_quant_pa_kernel(
                     nc.tensor.transpose(bank[:, col : col + 128], words[:, src + u : src + 256 : 2], ident[:])
 
         def scaled_sx(v, g, bank):
-            y = ep.tile([P, 1024], F32, tag=("t1", "t2")[v], name="y")
+            y = hp.tile([P, 1024], F32, tag="t1", name="y")
             for t in range(4):
                 i = 16 * v + 4 * g + t
                 nc.scalar.activation(
@@ -176,11 +194,29 @@ def tile_rwkv_timemix_for_quant_pa_kernel(
             sb = tp.tile([P, 512], F32, tag="tp", name="sb")
             transpose_group(sw, g, sb)
             sbank.append(sb)
-            xb = acc.tile([P, 512], F32, tag="acc", name="xb")
+            xb = acc.tile([P, 512], F32, tag="kv"[g // 2], name="xb")
             transpose_group(xw, g, xb)
             xbank.append(xb)
-        for v, g in ((0, 0), (0, 1), (1, 0), (0, 2), (1, 1), (0, 3), (1, 2), (1, 3)):
+        for v, g in ((0, 0), (0, 1), (1, 0)):
             mix(v, g, scaled_sx(v, g, sbank[g]))
+
+        BIG = 1e30
+        edec = const.tile([P, NT], F32, name="edec")
+        rest = const.tile([P, NT], F32, name="rest")
+        nc.scalar.activation(out=edec[:], in_=td_rows[:], func=ACT.Exp)
+        mix(0, 2, scaled_sx(0, 2, sbank[2]))
+        nc.vector.tensor_scalar_min(out=vec_rows[0:32, :], in0=edec[0:32, :], scalar1=BIG)
+        nc.vector.tensor_scalar_min(out=vec_rows[64:128, :], in0=edec[64:128, :], scalar1=BIG)
+        mix(1, 1, scaled_sx(1, 1, sbank[1]))
+        nc.vector.scalar_tensor_tensor(
+            out=rest[64:128, :], in0=edec[64:128, :], scalar=BIG, in1=vec_rows[64:128, :], op0=ALU.min, op1=ALU.subtract
+        )
+        mix(0, 3, scaled_sx(0, 3, sbank[3]))
+        nc.vector.tensor_copy(out=vec_rows[64:128, :], in_=rest[64:128, :])
+        mix(1, 2, scaled_sx(1, 2, sbank[2]))
+        nc.vector.tensor_tensor(out=rest[96:128, :], in0=rest[96:128, :], in1=vec_rows[96:128, :], op=ALU.subtract)
+        mix(1, 3, scaled_sx(1, 3, sbank[3]))
+        nc.vector.tensor_copy(out=vec_rows[96:128, :], in_=rest[96:128, :])
         load_w(1, 1, 0)
         load_w(1, 1, 1)
 
@@ -197,22 +233,25 @@ def tile_rwkv_timemix_for_quant_pa_kernel(
         def new_gt():
             return grp.tile([P, 8192], BF16, tag="grp", name="gt", align_bytes=64)
 
-        def regroup_w(v, j, gt, halves=(0, 1)):
+        def regroup_w(v, j, gt, banks, tags=()):
             gw = gt[:].bitcast(F32).rearrange("p (g d u) -> p g d u", g=4, d=NT, u=2)
-            for hb in halves:
-                for c in range(4):
-                    wf = raw_w[(v, j, c // 2)][:].bitcast(F32)
-                    base = 1024 * (c % 2)
+            for i, b in enumerate(banks):
+                hb, c = b // 4, b % 4
+                wf = raw_w[(v, j, c // 2)][:].bitcast(F32)
+                base = 1024 * (c % 2)
+                if i < len(tags) and tags[i] == "k":
+                    bank = acc.tile([P, 512], F32, tag="k", name="bank")
+                else:
                     bank = tp.tile([P, 512], F32, tag="tp", name="bank")
-                    for gi in range(2):
-                        for u in range(2):
-                            src = base + 256 * (2 * hb + gi)
-                            col = 128 * (2 * gi + u)
-                            nc.tensor.transpose(bank[:, col : col + 128], wf[:, src + u : src + 256 : 2], ident[:])
-                    nc.scalar.copy(
-                        out=gw[:, 2 * hb : 2 * hb + 2, 128 * c : 128 * (c + 1), :],
-                        in_=bank[:].rearrange("p (g u d) -> p g d u", g=2, u=2, d=128),
-                    )
+                for gi in range(2):
+                    for u in range(2):
+                        src = base + 256 * (2 * hb + gi)
+                        col = 128 * (2 * gi + u)
+                        nc.tensor.transpose(bank[:, col : col + 128], wf[:, src + u : src + 256 : 2], ident[:])
+                nc.scalar.copy(
+                    out=gw[:, 2 * hb : 2 * hb + 2, 128 * c : 128 * (c + 1), :],
+                    in_=bank[:].rearrange("p (g u d) -> p g d u", g=2, u=2, d=128),
+                )
 
         def new_codes():
             codes = cod.tile([P, 2048], U32, tag="codes", name="codes", align_bytes=64)
@@ -228,47 +267,25 @@ def tile_rwkv_timemix_for_quant_pa_kernel(
                     in_=gt[:, 4096 * hb : 4096 * (hb + 1)],
                 )
 
-        def project(v, wq, r):
+        def project(v, wq):
             codes, scl = wq
-            ps = acc.tile([P, NT], F32, tag="acc", name="ps")
+            ps = [acc.tile([P, NT], F32, tag="kv"[v], name="ps") for r in range(2)]
             for g in range(4):
-                c0 = 1024 * v + 256 * g + 128 * r
-                nc.tensor.matmul_mx(
-                    out=ps[:],
-                    lhsT=xcodes[:, c0 : c0 + 128].bitcast(FP8X4),
-                    lhsT_scale=xscl[:, c0 : c0 + 128],
-                    rhs=codes[:, NT * g : NT * (g + 1)].bitcast(FP8X4),
-                    rhs_scale=scl[:, NT * g : NT * (g + 1)],
-                    start=(g == 0),
-                    stop=(g == 3),
-                )
+                for r in range(2):
+                    c0 = 1024 * v + 256 * g + 128 * r
+                    nc.tensor.matmul_mx(
+                        out=ps[r][:],
+                        lhsT=xcodes[:, c0 : c0 + 128].bitcast(FP8X4),
+                        lhsT_scale=xscl[:, c0 : c0 + 128],
+                        rhs=codes[:, NT * g : NT * (g + 1)].bitcast(FP8X4),
+                        rhs_scale=scl[:, NT * g : NT * (g + 1)],
+                        start=(g == 0),
+                        stop=(g == 3),
+                    )
             return ps
 
-        delta = const.tile([P, D], F32, name="delta")
         h_tiles = {}
-        spread = {}
-
-        def row_spread(j, row, name):
-            ps = tp.tile([P, NT], F32, tag="tp", name=name)
-            nc.tensor.matmul(
-                out=ps[:],
-                lhsT=identb[:, row : row + 1].to_broadcast([P, P]),
-                rhs=vec_rows[:, NT * j : NT * (j + 1)],
-                start=True,
-                stop=True,
-            )
-            return ps
-
-        def spread_vectors(j):
-            tf_ps = row_spread(j, 0, "tf_ps")
-            td_ps = row_spread(j, 1, "td_ps")
-            etd = ep.tile([P, NT], F32, tag="etd", name="etd")
-            nc.scalar.activation(out=etd[:], in_=td_ps[:], func=ACT.Exp)
-            spread[j] = (tf_ps, etd)
-
-        def make_delta(j):
-            tf_ps, etd = spread[j]
-            nc.vector.tensor_tensor(out=delta[:, NT * j : NT * (j + 1)], in0=tf_ps[:], in1=etd[:], op=ALU.subtract)
+        delta = {}
 
         def make_h(j):
             h_tiles[j] = []
@@ -279,14 +296,18 @@ def tile_rwkv_timemix_for_quant_pa_kernel(
                 )
                 nc.tensor.matmul(
                     out=ps[:],
-                    lhsT=nidentb[:, 0:1].to_broadcast([P, P]),
-                    rhs=vec_rows[:, NT * j : NT * (j + 1)],
+                    lhsT=nidentb[:, 32 + j : 33 + j].to_broadcast([P, P]),
+                    rhs=vec_rows[:],
                     start=False,
                     stop=True,
                 )
                 h = hp.tile([P, NT], F32, tag="h", name="h")
                 nc.scalar.copy(out=h[:], in_=ps[:])
                 h_tiles[j].append(h)
+            delta[j] = dl.tile([P, NT], F32, tag="dl", name="delta")
+            nc.tensor.matmul(
+                out=delta[j][:], lhsT=sel[:, j : j + 1].to_broadcast([P, P]), rhs=vec_rows[:], start=True, stop=True
+            )
 
         two = "p (h d) -> p h d"
 
@@ -310,7 +331,7 @@ def tile_rwkv_timemix_for_quant_pa_kernel(
                 nc.vector.tensor_tensor(
                     out=ndd[r][:, NT : 2 * NT],
                     in0=ndd[r][:, 0:NT],
-                    in1=delta[:, NT * j : NT * (j + 1)],
+                    in1=delta[j][:],
                     op=ALU.add,
                 )
             for r in range(2):
@@ -326,7 +347,7 @@ def tile_rwkv_timemix_for_quant_pa_kernel(
 
         def state_terms(j, xf1):
             a_t, b_t = states[j][1], states[j][2]
-            t1 = [ep.tile([P, 1024], F32, tag="t1", name="t1") for r in range(2)]
+            t1 = [hp.tile([P, 1024], F32, tag="t1", name="t1") for r in range(2)]
             for r in range(2):
                 nc.vector.scalar_tensor_tensor(
                     out=t1[r][:].rearrange(two, h=2),
@@ -374,54 +395,55 @@ def tile_rwkv_timemix_for_quant_pa_kernel(
 
         gt_k, gt_v = new_gt(), new_gt()
         wq_k, wq_v = new_codes(), new_codes()
-        regroup_w(0, 0, gt_k)
+        regroup_w(0, 0, gt_k, range(8))
         load_states(1)
-        spread_vectors(0)
+        load_w(0, 2, 0)
+        load_w(0, 2, 1)
         make_h(0)
         quantise_x(0)
         quantise_w(gt_k, wq_k)
-        make_delta(0)
-        regroup_w(1, 0, gt_v, (0,))
-        k_ps = [project(0, wq_k, r) for r in range(2)]
-        regroup_w(1, 0, gt_v, (1,))
+        regroup_w(1, 0, gt_v, range(4))
+        k_ps = project(0, wq_k)
         quantise_x(1)
-        quantise_w(gt_v, wq_v, (0,))
+        regroup_w(1, 0, gt_v, range(4, 8))
         xf1, xf2 = exponents(0, k_ps)
-        quantise_w(gt_v, wq_v, (1,))
-        v_ps = [project(1, wq_v, r) for r in range(2)]
+        load_w(1, 2, 0)
+        load_w(1, 2, 1)
 
         for j in range(TILES):
             last = j + 1 == TILES
-            if j > 0:
-                xf1, xf2 = exponents(j, k_ps)
-                numerator(j - 1, 1, t1[1], t2[1], nc.vector)
-            if j + 2 < TILES:
-                load_w(0, j + 2, 0)
-                load_w(0, j + 2, 1)
+            quantise_w(gt_v, wq_v)
             if not last:
-                gt_k, gt_v = new_gt(), new_gt()
-                regroup_w(0, j + 1, gt_k)
-                regroup_w(1, j + 1, gt_v)
-                spread_vectors(j + 1)
                 make_h(j + 1)
+                gt_k = new_gt()
+                regroup_w(0, j + 1, gt_k, range(3), "tkk")
             t1 = state_terms(j, xf1)
+            v_ps = project(1, wq_v)
+            if not last:
+                regroup_w(0, j + 1, gt_k, range(3, 8))
+                gt_v = new_gt()
+                regroup_w(1, j + 1, gt_v, range(4))
+                if j == 0:
+                    load_w(0, 3, 0)
+                    load_w(0, 3, 1)
             denominators(j, xf1, xf2)
             if j + 2 < TILES:
-                load_w(1, j + 2, 0)
-                load_w(1, j + 2, 1)
                 load_states(j + 2)
             if not last:
                 wq_k, wq_v = new_codes(), new_codes()
                 quantise_w(gt_k, wq_k)
-                k_ps = [project(0, wq_k, r) for r in range(2)]
-                quantise_w(gt_v, wq_v)
-            t2 = [value_term(j, v_ps, xf2, 0)]
-            if not last:
-                numerator(j, 0, t1[0], t2[0], nc.gpsimd)
-            t2.append(value_term(j, v_ps, xf2, 1))
-            if not last:
-                make_delta(j + 1)
-                v_ps = [project(1, wq_v, r) for r in range(2)]
-            else:
+                k_ps = project(0, wq_k)
+                regroup_w(1, j + 1, gt_v, range(4, 8))
+                if j == 0:
+                    load_w(1, 3, 0)
+                    load_w(1, 3, 1)
+            t2 = []
+            for r in range(2):
+                t2.append(value_term(j, v_ps, xf2, r))
+                if not last:
+                    numerator(j, r, t1[r], t2[r], nc.gpsimd)
+            if last:
                 for r in range(2):
                     numerator(j, r, t1[r], t2[r], nc.vector)
+            else:
+                xf1, xf2 = exponents(j + 1, k_ps)

@@ -18,6 +18,7 @@ D = 2048
 NT = 512
 TILES = D // NT
 FLOPS = 2 * 2 * ROWS * E * D
+BIG = 1e30
 
 
 def tile_rwkv_timemix_for_quant_pa_kernel(
@@ -48,8 +49,7 @@ def tile_rwkv_timemix_for_quant_pa_kernel(
         st = ctx.enter_context(tc.tile_pool(name="st", bufs=2))
         ep = ctx.enter_context(tc.tile_pool(name="ep", bufs=2))
         hp = ctx.enter_context(tc.tile_pool(name="hp", bufs=4))
-        dl = ctx.enter_context(tc.psum_pool(name="dl", bufs=1))
-        tp = ctx.enter_context(tc.psum_pool(name="tp", bufs=3))
+        tp = ctx.enter_context(tc.psum_pool(name="tp", bufs=4))
         acc = ctx.enter_context(tc.psum_pool(name="acc", bufs=2))
         ctx.enter_context(tc.manual_schedule())
 
@@ -57,14 +57,15 @@ def tile_rwkv_timemix_for_quant_pa_kernel(
         raw_w = {}
         states = {}
 
-        def load_w(v, j, h):
-            wr = ring.tile([P, 4096], BF16, tag="ring", name="wr")
-            row0 = NT * j + 256 * h
-            nc.sync.dma_start(
-                out=wr[:].rearrange("p (c k) -> p c k", c=2),
-                in_=weights[v][row0 : row0 + 256, :].rearrange("(c p) k -> p c k", p=P),
-            )
-            raw_w[(v, j, h)] = wr
+        def load_w(v, j):
+            for h in range(2):
+                wr = ring.tile([P, 4096], BF16, tag="ring", name="wr")
+                row0 = NT * j + 256 * h
+                nc.sync.dma_start(
+                    out=wr[:].rearrange("p (c k) -> p c k", c=2),
+                    in_=weights[v][row0 : row0 + 256, :].rearrange("(c p) k -> p c k", p=P),
+                )
+                raw_w[(v, j, h)] = wr
 
         def load_state(j, i):
             src = (state_p, state_A, state_B)[i]
@@ -84,28 +85,16 @@ def tile_rwkv_timemix_for_quant_pa_kernel(
         nc.vector.memset(warm_in[:], 0.0)
         mkb = const.tile([P, 32], BF16, name="mkb")
         with nc.allow_non_contiguous_dma(reason="mix coefficients, four neighbouring k to a partition"):
-            nc.scalar.dma_start(
-                out=mkb[:, 0:16].rearrange("p (g t) -> p g t", t=4),
-                in_=time_mix_k.rearrange("o (g p t) -> p (o g) t", g=4, p=P, t=4),
-            )
-            nc.scalar.dma_start(
-                out=mkb[:, 16:32].rearrange("p (g t) -> p g t", t=4),
-                in_=time_mix_v.rearrange("o (g p t) -> p (o g) t", g=4, p=P, t=4),
-            )
+            for v, src in enumerate((time_mix_k, time_mix_v)):
+                nc.scalar.dma_start(
+                    out=mkb[:, 16 * v : 16 * (v + 1)].rearrange("p (g t) -> p g t", t=4),
+                    in_=src.rearrange("o (g p t) -> p (o g) t", g=4, p=P, t=4),
+                )
         nc.scalar.activation(out=warm_out[:], in_=warm_in[:], func=ACT.Exp)
         td_rows = const.tile([P, NT], BF16, name="td_rows")
         vec_rows = const.tile([P, NT], BF16, name="vec_rows")
         nc.vector.memset(td_rows[:], 0.0)
         nc.vector.memset(vec_rows[:], 0.0)
-        nc.scalar.activation(out=warm_out[:], in_=warm_in[:], func=ACT.Exp)
-        td_rows = const.tile([P, NT], BF16, name="td_rows")
-        vec_rows = const.tile([P, NT], BF16, name="vec_rows")
-        nc.vector.memset(td_rows[:], 0.0)
-        nc.vector.memset(vec_rows[:], 0.0)
-        for row in (0, 64, 96):
-            nc.scalar.dma_start(out=td_rows[row : row + TILES, :], in_=time_decay.rearrange("(j d) -> j d", j=TILES))
-        nc.scalar.dma_start(out=vec_rows[32 : 32 + TILES, :], in_=time_first.rearrange("(j d) -> j d", j=TILES))
-        nc.scalar.activation(out=warm_out[:], in_=warm_in[:], func=ACT.Exp)
         x_sb = ring.tile([P, 4096], BF16, tag="ring", name="x_sb")
         sx_sb = ring.tile([P, 4096], BF16, tag="ring", name="sx_sb")
         for g in range(4):
@@ -114,14 +103,15 @@ def tile_rwkv_timemix_for_quant_pa_kernel(
                     out=dst[:, 1024 * g : 1024 * (g + 1)].rearrange("p (r k) -> p r k", r=2),
                     in_=src.rearrange("(r p) k -> p r k", p=P)[:, :, 512 * g : 512 * (g + 1)],
                 )
+        for row in (0, 64, 96):
+            nc.sync.dma_start(out=td_rows[row : row + TILES, :], in_=time_decay.rearrange("(j d) -> j d", j=TILES))
+        nc.sync.dma_start(out=vec_rows[32 : 32 + TILES, :], in_=time_first.rearrange("(j d) -> j d", j=TILES))
+        load_w(0, 0)
+        load_w(1, 0)
         load_state(0, 0)
-        for v in range(2):
-            for h in range(2):
-                load_w(v, 0, h)
         load_state(0, 1)
         load_state(0, 2)
-        load_w(0, 1, 0)
-        load_w(0, 1, 1)
+        load_w(0, 1)
 
         ident = const.tile([P, P], F32, name="ident")
         make_identity(nc, ident[:])
@@ -136,49 +126,12 @@ def tile_rwkv_timemix_for_quant_pa_kernel(
         mkf = const.tile([P, 32], F32, name="mkf")
         nc.vector.tensor_copy(out=mkf[:], in_=mkb[:])
 
-        omk = const.tile([P, 32], F32, name="omk")
-        nc.vector.tensor_scalar(out=omk[:], in0=mkf[:], scalar1=-1.0, scalar2=1.0, op0=ALU.mult, op1=ALU.add)
-
         xg = grp.tile([P, 8192], BF16, tag="grp", name="xg", align_bytes=64)
+        edec = const.tile([P, NT], F32, name="edec")
+        rest = const.tile([P, NT], F32, name="rest")
         sw = sx_sb[:].bitcast(F32)
-        xw = x_sb[:].bitcast(F32)
-        xbank = []
 
-        def of_t(bank, t):
-            half = bank[:, 512 * (t // 2) : 512 * (t // 2 + 1)]
-            return half.rearrange("p (n e) -> p n e", e=2)[:, :, t % 2]
-
-        def transpose_group(words, g, bank):
-            for u in range(2):
-                for r in range(2):
-                    src = 512 * g + 256 * r
-                    col = 256 * u + 128 * r
-                    nc.tensor.transpose(bank[:, col : col + 128], words[:, src + u : src + 256 : 2], ident[:])
-
-        def scaled_sx(v, g, bank):
-            y = hp.tile([P, 1024], F32, tag="t1", name="y")
-            for t in range(4):
-                i = 16 * v + 4 * g + t
-                nc.scalar.activation(
-                    out=y[:, 256 * t : 256 * (t + 1)],
-                    in_=of_t(bank[:].bitcast(BF16), t),
-                    func=ACT.Copy,
-                    scale=omk[:, i : i + 1],
-                )
-            return y
-
-        def mix(v, g, y):
-            pln = hp.tile([P, 1024], BF16, tag="hp", name="pln")
-            for t in range(4):
-                i = 16 * v + 4 * g + t
-                nc.vector.scalar_tensor_tensor(
-                    out=pln[:, 256 * t : 256 * (t + 1)],
-                    in0=of_t(xbank[g][:].bitcast(BF16), t),
-                    scalar=mkf[:, i : i + 1],
-                    in1=y[:, 256 * t : 256 * (t + 1)],
-                    op0=ALU.mult,
-                    op1=ALU.add,
-                )
+        def regroup_x(v, g, pln):
             o0 = 4096 * v + 1024 * g
             nc.gpsimd.tensor_scalar(
                 out=xg[:, o0 : o0 + 1024].rearrange("p (n t) -> p n t", t=4),
@@ -189,36 +142,65 @@ def tile_rwkv_timemix_for_quant_pa_kernel(
                 op1=ALU.add,
             )
 
-        sbank = []
+        def split_decay(step):
+            if step == 0:
+                nc.vector.tensor_scalar_min(out=vec_rows[0:32, :], in0=edec[0:32, :], scalar1=BIG)
+                nc.vector.tensor_scalar_min(out=vec_rows[64:128, :], in0=edec[64:128, :], scalar1=BIG)
+            elif step == 1:
+                nc.vector.scalar_tensor_tensor(
+                    out=rest[64:128, :],
+                    in0=edec[64:128, :],
+                    scalar=BIG,
+                    in1=vec_rows[64:128, :],
+                    op0=ALU.min,
+                    op1=ALU.subtract,
+                )
+            elif step == 2:
+                nc.vector.tensor_copy(out=vec_rows[64:128, :], in_=rest[64:128, :])
+            elif step == 3:
+                nc.vector.tensor_tensor(
+                    out=rest[96:128, :], in0=rest[96:128, :], in1=vec_rows[96:128, :], op=ALU.subtract
+                )
+            else:
+                nc.vector.tensor_copy(out=vec_rows[96:128, :], in_=rest[96:128, :])
+
         for g in range(4):
             sb = tp.tile([P, 512], F32, tag="tp", name="sb")
-            transpose_group(sw, g, sb)
-            sbank.append(sb)
-            xb = acc.tile([P, 512], F32, tag="kv"[g // 2], name="xb")
-            transpose_group(xw, g, xb)
-            xbank.append(xb)
-        for v, g in ((0, 0), (0, 1), (1, 0)):
-            mix(v, g, scaled_sx(v, g, sbank[g]))
-
-        BIG = 1e30
-        edec = const.tile([P, NT], F32, name="edec")
-        rest = const.tile([P, NT], F32, name="rest")
-        nc.scalar.activation(out=edec[:], in_=td_rows[:], func=ACT.Exp)
-        mix(0, 2, scaled_sx(0, 2, sbank[2]))
-        nc.vector.tensor_scalar_min(out=vec_rows[0:32, :], in0=edec[0:32, :], scalar1=BIG)
-        nc.vector.tensor_scalar_min(out=vec_rows[64:128, :], in0=edec[64:128, :], scalar1=BIG)
-        mix(1, 1, scaled_sx(1, 1, sbank[1]))
-        nc.vector.scalar_tensor_tensor(
-            out=rest[64:128, :], in0=edec[64:128, :], scalar=BIG, in1=vec_rows[64:128, :], op0=ALU.min, op1=ALU.subtract
-        )
-        mix(0, 3, scaled_sx(0, 3, sbank[3]))
-        nc.vector.tensor_copy(out=vec_rows[64:128, :], in_=rest[64:128, :])
-        mix(1, 2, scaled_sx(1, 2, sbank[2]))
-        nc.vector.tensor_tensor(out=rest[96:128, :], in0=rest[96:128, :], in1=vec_rows[96:128, :], op=ALU.subtract)
-        mix(1, 3, scaled_sx(1, 3, sbank[3]))
-        nc.vector.tensor_copy(out=vec_rows[96:128, :], in_=rest[96:128, :])
-        load_w(1, 1, 0)
-        load_w(1, 1, 1)
+            for u in range(2):
+                for r in range(2):
+                    src = 512 * g + 256 * r
+                    col = 256 * u + 128 * r
+                    nc.tensor.transpose(sb[:, col : col + 128], sw[:, src + u : src + 256 : 2], ident[:])
+            sxs = ep.tile([P, 1024], BF16, tag="ndd", name="sxs")
+            nc.scalar.copy(out=sxs[:].bitcast(F32), in_=sb[:])
+            if g == 2:
+                nc.scalar.activation(out=edec[:], in_=td_rows[:], func=ACT.Exp)
+            plns = [hp.tile([P, 1024], BF16, tag="hp", name="pln") for v in range(2)]
+            for u in range(2):
+                dxb = acc.tile([P, 512], F32, tag="kv"[u], name="dxb")
+                for e in range(2):
+                    for r in range(2):
+                        base = 1024 * g + 512 * r
+                        col = 256 * e + 128 * r
+                        xs = x_sb[:, base : base + 512].rearrange("p (w t) -> p w t", t=4)[:, :, 2 * u + e]
+                        ss = sx_sb[:, base : base + 512].rearrange("p (w t) -> p w t", t=4)[:, :, 2 * u + e]
+                        nc.tensor.matmul(out=dxb[:, col : col + 128], lhsT=xs, rhs=identb[:], start=True, stop=False)
+                        nc.tensor.matmul(out=dxb[:, col : col + 128], lhsT=ss, rhs=nidentb[:], start=False, stop=True)
+                for v in range(2):
+                    for e in range(2):
+                        t = 2 * u + e
+                        i = 16 * v + 4 * g + t
+                        nc.vector.scalar_tensor_tensor(
+                            out=plns[v][:, 256 * t : 256 * (t + 1)],
+                            in0=dxb[:, 256 * e : 256 * (e + 1)],
+                            scalar=mkf[:, i : i + 1],
+                            in1=sxs[:, 512 * u : 512 * (u + 1)].rearrange("p (n e) -> p n e", e=2)[:, :, e],
+                            op0=ALU.mult,
+                            op1=ALU.add,
+                        )
+            for v in range(2):
+                regroup_x(v, g, plns[v])
+        load_w(1, 1)
 
         xcodes = const.tile([P, 2048], U32, name="xcodes", align_bytes=64)
         xscl = const.tile([P, 2048], U8, name="xscl", align_bytes=64)
@@ -267,10 +249,12 @@ def tile_rwkv_timemix_for_quant_pa_kernel(
                     in_=gt[:, 4096 * hb : 4096 * (hb + 1)],
                 )
 
-        def project(v, wq):
+        def new_ps(v):
+            return [acc.tile([P, NT], F32, tag="kv"[v], name="ps") for r in range(2)]
+
+        def project(v, wq, ps, groups=range(4)):
             codes, scl = wq
-            ps = [acc.tile([P, NT], F32, tag="kv"[v], name="ps") for r in range(2)]
-            for g in range(4):
+            for g in groups:
                 for r in range(2):
                     c0 = 1024 * v + 256 * g + 128 * r
                     nc.tensor.matmul_mx(
@@ -282,32 +266,15 @@ def tile_rwkv_timemix_for_quant_pa_kernel(
                         start=(g == 0),
                         stop=(g == 3),
                     )
-            return ps
 
-        h_tiles = {}
-        delta = {}
+        rows_ps = {}
 
-        def make_h(j):
-            h_tiles[j] = []
-            for r in range(2):
-                ps = tp.tile([P, NT], F32, tag="tp", name="h_ps")
-                nc.tensor.matmul(
-                    out=ps[:], lhsT=identb[:], rhs=states[j][0][:, NT * r : NT * (r + 1)], start=True, stop=False
-                )
-                nc.tensor.matmul(
-                    out=ps[:],
-                    lhsT=nidentb[:, 32 + j : 33 + j].to_broadcast([P, P]),
-                    rhs=vec_rows[:],
-                    start=False,
-                    stop=True,
-                )
-                h = hp.tile([P, NT], F32, tag="h", name="h")
-                nc.scalar.copy(out=h[:], in_=ps[:])
-                h_tiles[j].append(h)
-            delta[j] = dl.tile([P, NT], F32, tag="dl", name="delta")
-            nc.tensor.matmul(
-                out=delta[j][:], lhsT=sel[:, j : j + 1].to_broadcast([P, P]), rhs=vec_rows[:], start=True, stop=True
-            )
+        def spread_rows(j):
+            rows_ps[j] = []
+            for cols in (identb[:, 32 + j : 33 + j], sel[:, j : j + 1]):
+                ps = tp.tile([P, NT], F32, tag="tp", name="row_ps")
+                nc.tensor.matmul(out=ps[:], lhsT=cols.to_broadcast([P, P]), rhs=vec_rows[:], start=True, stop=True)
+                rows_ps[j].append(ps)
 
         two = "p (h d) -> p h d"
 
@@ -321,19 +288,19 @@ def tile_rwkv_timemix_for_quant_pa_kernel(
             return ap.unsqueeze(1).to_broadcast([P, 2, NT])
 
         def exponents(j, k_ps):
+            sp_t = states[j][0]
+            tf_ps, delta = rows_ps[j]
+            nq = [hp.tile([P, NT], F32, tag="hp", name="nq") for r in range(2)]
             ndd = [ep.tile([P, 1024], F32, tag="ndd", name="ndd") for r in range(2)]
             xf1 = [ep.tile([P, 1024], F32, tag="xf0", name="xf1") for r in range(2)]
             xf2 = [ep.tile([P, 1024], F32, tag="xf1", name="xf2") for r in range(2)]
             p2 = [ep.tile([P, NT], F32, tag="p2", name="p2") for r in range(2)]
             for r in range(2):
-                nc.vector.tensor_tensor(out=ndd[r][:, 0:NT], in0=h_tiles[j][r][:], in1=k_ps[r][:], op=ALU.subtract)
+                nc.vector.tensor_tensor(out=nq[r][:], in0=per_row_tile(sp_t, r), in1=k_ps[r][:], op=ALU.subtract)
             for r in range(2):
-                nc.vector.tensor_tensor(
-                    out=ndd[r][:, NT : 2 * NT],
-                    in0=ndd[r][:, 0:NT],
-                    in1=delta[j][:],
-                    op=ALU.add,
-                )
+                nc.vector.tensor_tensor(out=ndd[r][:, 0:NT], in0=nq[r][:], in1=tf_ps[:], op=ALU.subtract)
+            for r in range(2):
+                nc.vector.tensor_tensor(out=ndd[r][:, NT : 2 * NT], in0=ndd[r][:, 0:NT], in1=delta[:], op=ALU.add)
             for r in range(2):
                 nc.scalar.activation(out=xf1[r][:], in_=ndd[r][:], func=ACT.Exp)
             for r in range(2):
@@ -380,8 +347,8 @@ def tile_rwkv_timemix_for_quant_pa_kernel(
             )
             return t2
 
-        def denominators(j, xf1, xf2):
-            for r in range(2):
+        def denominators(j, xf1, xf2, rows=(0, 1)):
+            for r in rows:
                 nc.vector.scalar_tensor_tensor(
                     out=xf1[r][:], in0=xf2[r][:], scalar=1.0, in1=xf1[r][:], op0=ALU.min, op1=ALU.add
                 )
@@ -397,46 +364,51 @@ def tile_rwkv_timemix_for_quant_pa_kernel(
         wq_k, wq_v = new_codes(), new_codes()
         regroup_w(0, 0, gt_k, range(8))
         load_states(1)
-        load_w(0, 2, 0)
-        load_w(0, 2, 1)
-        make_h(0)
+        load_w(0, 2)
         quantise_x(0)
-        quantise_w(gt_k, wq_k)
-        regroup_w(1, 0, gt_v, range(4))
-        k_ps = project(0, wq_k)
+        split_decay(0)
+        quantise_w(gt_k, wq_k, (0,))
+        split_decay(1)
+        quantise_w(gt_k, wq_k, (1,))
+        split_decay(2)
+        regroup_w(1, 0, gt_v, range(3))
+        k_ps = new_ps(0)
+        project(0, wq_k, k_ps)
         quantise_x(1)
-        regroup_w(1, 0, gt_v, range(4, 8))
+        split_decay(3)
+        split_decay(4)
+        spread_rows(0)
+        regroup_w(1, 0, gt_v, range(3, 8))
         xf1, xf2 = exponents(0, k_ps)
-        load_w(1, 2, 0)
-        load_w(1, 2, 1)
+        load_w(1, 2)
 
         for j in range(TILES):
             last = j + 1 == TILES
             quantise_w(gt_v, wq_v)
             if not last:
-                make_h(j + 1)
                 gt_k = new_gt()
                 regroup_w(0, j + 1, gt_k, range(3), "tkk")
             t1 = state_terms(j, xf1)
-            v_ps = project(1, wq_v)
+            v_ps = new_ps(1)
+            project(1, wq_v, v_ps)
             if not last:
                 regroup_w(0, j + 1, gt_k, range(3, 8))
                 gt_v = new_gt()
                 regroup_w(1, j + 1, gt_v, range(4))
                 if j == 0:
-                    load_w(0, 3, 0)
-                    load_w(0, 3, 1)
+                    load_w(0, 3)
             denominators(j, xf1, xf2)
             if j + 2 < TILES:
                 load_states(j + 2)
             if not last:
                 wq_k, wq_v = new_codes(), new_codes()
                 quantise_w(gt_k, wq_k)
-                k_ps = project(0, wq_k)
+                k_ps = new_ps(0)
+                project(0, wq_k, k_ps)
+                spread_rows(j + 1)
                 regroup_w(1, j + 1, gt_v, range(4, 8))
                 if j == 0:
-                    load_w(1, 3, 0)
-                    load_w(1, 3, 1)
+                    load_w(1, 3)
             t2 = []
             for r in range(2):
                 t2.append(value_term(j, v_ps, xf2, r))

@@ -18,7 +18,7 @@ D = 2048
 NT = 512
 TILES = D // NT
 FLOPS = 2 * 2 * ROWS * E * D
-BIG = 1e30
+TD_MAX = 69.0
 
 
 def tile_rwkv_timemix_for_quant_pa_kernel(
@@ -74,11 +74,7 @@ def tile_rwkv_timemix_for_quant_pa_kernel(
                 out=t[:].rearrange("p (r d) -> p r d", r=2),
                 in_=src.rearrange("(r p) d -> p r d", p=P)[:, :, NT * j : NT * (j + 1)],
             )
-            states.setdefault(j, []).append(t)
-
-        def load_states(j):
-            for i in range(3):
-                load_state(j, i)
+            states[(j, i)] = t
 
         warm_in = const.tile([P, 1], F32, name="warm_in")
         warm_out = const.tile([P, 1], F32, name="warm_out")
@@ -91,10 +87,10 @@ def tile_rwkv_timemix_for_quant_pa_kernel(
                     in_=src.rearrange("o (g p t) -> p (o g) t", g=4, p=P, t=4),
                 )
         nc.scalar.activation(out=warm_out[:], in_=warm_in[:], func=ACT.Exp)
-        td_rows = const.tile([P, NT], BF16, name="td_rows")
         vec_rows = const.tile([P, NT], BF16, name="vec_rows")
-        nc.vector.memset(td_rows[:], 0.0)
         nc.vector.memset(vec_rows[:], 0.0)
+        vec_rows_f = const.tile([P, NT], F32, name="vec_rows_f")
+        nc.vector.memset(vec_rows_f[:], 0.0)
         x_sb = ring.tile([P, 4096], BF16, tag="ring", name="x_sb")
         sx_sb = ring.tile([P, 4096], BF16, tag="ring", name="sx_sb")
         for g in range(4):
@@ -103,14 +99,12 @@ def tile_rwkv_timemix_for_quant_pa_kernel(
                     out=dst[:, 1024 * g : 1024 * (g + 1)].rearrange("p (r k) -> p r k", r=2),
                     in_=src.rearrange("(r p) k -> p r k", p=P)[:, :, 512 * g : 512 * (g + 1)],
                 )
-        for row in (0, 64, 96):
-            nc.sync.dma_start(out=td_rows[row : row + TILES, :], in_=time_decay.rearrange("(j d) -> j d", j=TILES))
-        nc.sync.dma_start(out=vec_rows[32 : 32 + TILES, :], in_=time_first.rearrange("(j d) -> j d", j=TILES))
+        for row, src in ((0, time_decay), (32, time_first)):
+            nc.sync.dma_start(out=vec_rows[row : row + TILES, :], in_=src.rearrange("(j d) -> j d", j=TILES))
         load_w(0, 0)
         load_w(1, 0)
-        load_state(0, 0)
-        load_state(0, 1)
-        load_state(0, 2)
+        for i in range(3):
+            load_state(0, i)
         load_w(0, 1)
 
         ident = const.tile([P, P], F32, name="ident")
@@ -119,63 +113,50 @@ def tile_rwkv_timemix_for_quant_pa_kernel(
         make_identity(nc, identb[:])
         nidentb = const.tile([P, P], BF16, name="nidentb")
         nc.gpsimd.tensor_scalar(out=nidentb[:], in0=identb[:], scalar1=-1.0, scalar2=0.0, op0=ALU.mult, op1=ALU.add)
-        sel = const.tile([P, TILES], BF16, name="sel")
-        nc.gpsimd.tensor_tensor(out=sel[:], in0=identb[:, 32 : 32 + TILES], in1=identb[:, 0:TILES], op=ALU.subtract)
-        nc.gpsimd.tensor_tensor(out=sel[:], in0=sel[:], in1=identb[:, 64 : 64 + TILES], op=ALU.subtract)
-        nc.gpsimd.tensor_tensor(out=sel[:], in0=sel[:], in1=identb[:, 96 : 96 + TILES], op=ALU.subtract)
+        sel = const.tile([P, TILES], F32, name="sel")
+        nc.gpsimd.tensor_tensor(out=sel[:], in0=ident[:, 32 : 32 + TILES], in1=ident[:, 0:TILES], op=ALU.subtract)
         mkf = const.tile([P, 32], F32, name="mkf")
         nc.vector.tensor_copy(out=mkf[:], in_=mkb[:])
 
         xg = grp.tile([P, 8192], BF16, tag="grp", name="xg", align_bytes=64)
-        edec = const.tile([P, NT], F32, name="edec")
-        rest = const.tile([P, NT], F32, name="rest")
         sw = sx_sb[:].bitcast(F32)
 
-        def regroup_x(v, g, pln):
-            o0 = 4096 * v + 1024 * g
-            nc.gpsimd.tensor_scalar(
-                out=xg[:, o0 : o0 + 1024].rearrange("p (n t) -> p n t", t=4),
-                in0=pln[:].rearrange("p (t n) -> p n t", t=4),
-                scalar1=1.0,
-                scalar2=0.0,
-                op0=ALU.mult,
-                op1=ALU.add,
+        def regroup_key(g, pln):
+            out = xg[:, 1024 * g : 1024 * (g + 1)].rearrange("p (n t) -> p n t", t=4)
+            in_ = pln[:].rearrange("p (t n) -> p n t", t=4)
+            if g < 3:
+                nc.gpsimd.tensor_scalar(out=out, in0=in_, scalar1=1.0, scalar2=0.0, op0=ALU.mult, op1=ALU.add)
+            else:
+                nc.vector.tensor_copy(out=out, in_=in_)
+
+        def add_value(g):
+            o0 = 4096 + 1024 * g
+            nc.vector.tensor_tensor(
+                out=xg[:, o0 : o0 + 1024].rearrange("p (n u e) -> p n u e", u=2, e=2),
+                in0=scaled[g][:].rearrange("p (u e n) -> p n u e", u=2, e=2),
+                in1=state_x_t[g][:].rearrange("p (u n e) -> p n u e", u=2, e=2),
+                op=ALU.add,
             )
 
-        def split_decay(step):
-            if step == 0:
-                nc.vector.tensor_scalar_min(out=vec_rows[0:32, :], in0=edec[0:32, :], scalar1=BIG)
-                nc.vector.tensor_scalar_min(out=vec_rows[64:128, :], in0=edec[64:128, :], scalar1=BIG)
-            elif step == 1:
-                nc.vector.scalar_tensor_tensor(
-                    out=rest[64:128, :],
-                    in0=edec[64:128, :],
-                    scalar=BIG,
-                    in1=vec_rows[64:128, :],
-                    op0=ALU.min,
-                    op1=ALU.subtract,
-                )
-            elif step == 2:
-                nc.vector.tensor_copy(out=vec_rows[64:128, :], in_=rest[64:128, :])
-            elif step == 3:
-                nc.vector.tensor_tensor(
-                    out=rest[96:128, :], in0=rest[96:128, :], in1=vec_rows[96:128, :], op=ALU.subtract
-                )
-            else:
-                nc.vector.tensor_copy(out=vec_rows[96:128, :], in_=rest[96:128, :])
+        state_x_t = {}
+        scaled = {}
 
-        for g in range(4):
+        def turn_state_x(g):
             sb = tp.tile([P, 512], F32, tag="tp", name="sb")
             for u in range(2):
                 for r in range(2):
                     src = 512 * g + 256 * r
                     col = 256 * u + 128 * r
                     nc.tensor.transpose(sb[:, col : col + 128], sw[:, src + u : src + 256 : 2], ident[:])
-            sxs = ep.tile([P, 1024], BF16, tag="ndd", name="sxs")
+            sxs = ep.tile([P, 1024], BF16, tag=("ndd", "xf0")[g % 2], name="sxs")
             nc.scalar.copy(out=sxs[:].bitcast(F32), in_=sb[:])
-            if g == 2:
-                nc.scalar.activation(out=edec[:], in_=td_rows[:], func=ACT.Exp)
-            plns = [hp.tile([P, 1024], BF16, tag="hp", name="pln") for v in range(2)]
+            state_x_t[g] = sxs
+
+        turn_state_x(0)
+        for g in range(4):
+            sxs = state_x_t[g]
+            pln = hp.tile([P, 1024], BF16, tag="p2", name="pln")
+            scaled[g] = hp.tile([P, 1024], F32, tag="t1", name="scaled")
             for u in range(2):
                 dxb = acc.tile([P, 512], F32, tag="kv"[u], name="dxb")
                 for e in range(2):
@@ -186,20 +167,35 @@ def tile_rwkv_timemix_for_quant_pa_kernel(
                         ss = sx_sb[:, base : base + 512].rearrange("p (w t) -> p w t", t=4)[:, :, 2 * u + e]
                         nc.tensor.matmul(out=dxb[:, col : col + 128], lhsT=xs, rhs=identb[:], start=True, stop=False)
                         nc.tensor.matmul(out=dxb[:, col : col + 128], lhsT=ss, rhs=nidentb[:], start=False, stop=True)
-                for v in range(2):
-                    for e in range(2):
-                        t = 2 * u + e
-                        i = 16 * v + 4 * g + t
-                        nc.vector.scalar_tensor_tensor(
-                            out=plns[v][:, 256 * t : 256 * (t + 1)],
-                            in0=dxb[:, 256 * e : 256 * (e + 1)],
-                            scalar=mkf[:, i : i + 1],
-                            in1=sxs[:, 512 * u : 512 * (u + 1)].rearrange("p (n e) -> p n e", e=2)[:, :, e],
-                            op0=ALU.mult,
-                            op1=ALU.add,
-                        )
-            for v in range(2):
-                regroup_x(v, g, plns[v])
+                if u == 1 and g < 3:
+                    turn_state_x(g + 1)
+                for e in range(2):
+                    t = 2 * u + e
+                    i = 4 * g + t
+                    nc.vector.scalar_tensor_tensor(
+                        out=pln[:, 256 * t : 256 * (t + 1)],
+                        in0=dxb[:, 256 * e : 256 * (e + 1)],
+                        scalar=mkf[:, i : i + 1],
+                        in1=sxs[:, 512 * u : 512 * (u + 1)].rearrange("p (n e) -> p n e", e=2)[:, :, e],
+                        op0=ALU.mult,
+                        op1=ALU.add,
+                    )
+                for e in range(2):
+                    t = 2 * u + e
+                    i = 16 + 4 * g + t
+                    nc.scalar.activation(
+                        out=scaled[g][:, 256 * t : 256 * (t + 1)],
+                        in_=dxb[:, 256 * e : 256 * (e + 1)],
+                        func=ACT.Copy,
+                        scale=mkf[:, i : i + 1],
+                    )
+            regroup_key(g, pln)
+            if g == 0:
+                nc.gpsimd.tensor_scalar(
+                    out=vec_rows[0:32, :], in0=vec_rows[0:32, :], scalar1=TD_MAX, scalar2=0.0, op0=ALU.min, op1=ALU.add
+                )
+            if 0 < g < 3:
+                add_value(g - 1)
         load_w(1, 1)
 
         xcodes = const.tile([P, 2048], U32, name="xcodes", align_bytes=64)
@@ -270,11 +266,15 @@ def tile_rwkv_timemix_for_quant_pa_kernel(
         rows_ps = {}
 
         def spread_rows(j):
-            rows_ps[j] = []
-            for cols in (identb[:, 32 + j : 33 + j], sel[:, j : j + 1]):
-                ps = tp.tile([P, NT], F32, tag="tp", name="row_ps")
-                nc.tensor.matmul(out=ps[:], lhsT=cols.to_broadcast([P, P]), rhs=vec_rows[:], start=True, stop=True)
-                rows_ps[j].append(ps)
+            first = acc.tile([P, NT], F32, tag="v", name="first")
+            nc.tensor.matmul(
+                out=first[:], lhsT=identb[:, 32 + j : 33 + j].to_broadcast([P, P]), rhs=vec_rows[:], start=True, stop=True
+            )
+            delta = acc.tile([P, NT], F32, tag="v", name="delta")
+            nc.tensor.matmul(
+                out=delta[:], lhsT=sel[:, j : j + 1].to_broadcast([P, P]), rhs=vec_rows_f[:], start=True, stop=True
+            )
+            rows_ps[j] = (first, delta)
 
         two = "p (h d) -> p h d"
 
@@ -288,17 +288,18 @@ def tile_rwkv_timemix_for_quant_pa_kernel(
             return ap.unsqueeze(1).to_broadcast([P, 2, NT])
 
         def exponents(j, k_ps):
-            sp_t = states[j][0]
-            tf_ps, delta = rows_ps[j]
-            nq = [hp.tile([P, NT], F32, tag="hp", name="nq") for r in range(2)]
+            first, delta = rows_ps[j]
             ndd = [ep.tile([P, 1024], F32, tag="ndd", name="ndd") for r in range(2)]
             xf1 = [ep.tile([P, 1024], F32, tag="xf0", name="xf1") for r in range(2)]
             xf2 = [ep.tile([P, 1024], F32, tag="xf1", name="xf2") for r in range(2)]
-            p2 = [ep.tile([P, NT], F32, tag="p2", name="p2") for r in range(2)]
+            p2 = [hp.tile([P, NT], F32, tag="p2", name="p2") for r in range(2)]
+            nq = [ep.tile([P, NT], F32, tag="nq", name="nq") for r in range(2)]
             for r in range(2):
-                nc.vector.tensor_tensor(out=nq[r][:], in0=per_row_tile(sp_t, r), in1=k_ps[r][:], op=ALU.subtract)
+                nc.vector.tensor_tensor(
+                    out=nq[r][:], in0=per_row_tile(states[(j, 0)], r), in1=k_ps[r][:], op=ALU.subtract
+                )
             for r in range(2):
-                nc.vector.tensor_tensor(out=ndd[r][:, 0:NT], in0=nq[r][:], in1=tf_ps[:], op=ALU.subtract)
+                nc.vector.tensor_tensor(out=ndd[r][:, 0:NT], in0=nq[r][:], in1=first[:], op=ALU.subtract)
             for r in range(2):
                 nc.vector.tensor_tensor(out=ndd[r][:, NT : 2 * NT], in0=ndd[r][:, 0:NT], in1=delta[:], op=ALU.add)
             for r in range(2):
@@ -313,7 +314,7 @@ def tile_rwkv_timemix_for_quant_pa_kernel(
             return xf1, xf2
 
         def state_terms(j, xf1):
-            a_t, b_t = states[j][1], states[j][2]
+            a_t, b_t = states[(j, 1)], states[(j, 2)]
             t1 = [hp.tile([P, 1024], F32, tag="t1", name="t1") for r in range(2)]
             for r in range(2):
                 nc.vector.scalar_tensor_tensor(
@@ -347,39 +348,46 @@ def tile_rwkv_timemix_for_quant_pa_kernel(
             )
             return t2
 
-        def denominators(j, xf1, xf2, rows=(0, 1)):
-            for r in rows:
+        def denominators(j, xf1, xf2):
+            for r in range(2):
+                b = hp.tile([P, 1024], F32, tag="t1", name="b")
                 nc.vector.scalar_tensor_tensor(
-                    out=xf1[r][:], in0=xf2[r][:], scalar=1.0, in1=xf1[r][:], op0=ALU.min, op1=ALU.add
+                    out=b[:], in0=xf2[r][:], scalar=1.0, in1=xf1[r][:], op0=ALU.min, op1=ALU.add
                 )
-                store(out_1, j, r, xf1[r][:, 0:NT])
-                store(out_3, j, r, xf1[r][:, NT : 2 * NT])
+                store(out_1, j, r, b[:, 0:NT])
+                store(out_3, j, r, b[:, NT : 2 * NT])
 
-        def numerator(j, r, t1, t2, engine):
-            engine.tensor_tensor(out=t2[:], in0=t1[:], in1=t2[:], op=ALU.add)
+        def numerator(j, r, t1, t2):
+            nc.gpsimd.tensor_tensor(out=t2[:], in0=t1[:], in1=t2[:], op=ALU.add)
             store(out_0, j, r, t2[:, 0:NT])
             store(out_2, j, r, t2[:, NT : 2 * NT])
+
+        def numerator_halves(j, r, t1, t2):
+            for h, dst in enumerate((out_0, out_2)):
+                cols = slice(NT * h, NT * (h + 1))
+                nc.vector.tensor_tensor(out=t2[:, cols], in0=t1[:, cols], in1=t2[:, cols], op=ALU.add)
+                store(dst, j, r, t2[:, cols])
 
         gt_k, gt_v = new_gt(), new_gt()
         wq_k, wq_v = new_codes(), new_codes()
         regroup_w(0, 0, gt_k, range(8))
-        load_states(1)
         load_w(0, 2)
         quantise_x(0)
-        split_decay(0)
         quantise_w(gt_k, wq_k, (0,))
-        split_decay(1)
+        add_value(2)
         quantise_w(gt_k, wq_k, (1,))
-        split_decay(2)
+        nc.scalar.activation(out=vec_rows_f[0:32, :], in_=vec_rows[0:32, :], func=ACT.Exp)
+        nc.scalar.copy(out=vec_rows_f[32:64, :], in_=vec_rows[32:64, :])
         regroup_w(1, 0, gt_v, range(3))
         k_ps = new_ps(0)
         project(0, wq_k, k_ps)
-        quantise_x(1)
-        split_decay(3)
-        split_decay(4)
         spread_rows(0)
+        add_value(3)
+        quantise_x(1)
         regroup_w(1, 0, gt_v, range(3, 8))
         xf1, xf2 = exponents(0, k_ps)
+        for i in range(3):
+            load_state(1, i)
         load_w(1, 2)
 
         for j in range(TILES):
@@ -395,27 +403,28 @@ def tile_rwkv_timemix_for_quant_pa_kernel(
                 regroup_w(0, j + 1, gt_k, range(3, 8))
                 gt_v = new_gt()
                 regroup_w(1, j + 1, gt_v, range(4))
-                if j == 0:
-                    load_w(0, 3)
             denominators(j, xf1, xf2)
+            if j == 0:
+                load_w(0, 3)
             if j + 2 < TILES:
-                load_states(j + 2)
+                for i in range(3):
+                    load_state(j + 2, i)
             if not last:
                 wq_k, wq_v = new_codes(), new_codes()
                 quantise_w(gt_k, wq_k)
                 k_ps = new_ps(0)
                 project(0, wq_k, k_ps)
-                spread_rows(j + 1)
-                regroup_w(1, j + 1, gt_v, range(4, 8))
-                if j == 0:
-                    load_w(1, 3)
             t2 = []
             for r in range(2):
                 t2.append(value_term(j, v_ps, xf2, r))
                 if not last:
-                    numerator(j, r, t1[r], t2[r], nc.gpsimd)
+                    numerator(j, r, t1[r], t2[r])
             if last:
                 for r in range(2):
-                    numerator(j, r, t1[r], t2[r], nc.vector)
+                    numerator_halves(j, r, t1[r], t2[r])
             else:
+                spread_rows(j + 1)
+                regroup_w(1, j + 1, gt_v, range(4, 8))
                 xf1, xf2 = exponents(j + 1, k_ps)
+                if j == 0:
+                    load_w(1, 3)

@@ -93,14 +93,19 @@ def tile_rwkv_timemix_for_quant_pa_kernel(
         nc.vector.memset(vec_rows_f[:], 0.0)
         x_sb = ring.tile([P, 4096], BF16, tag="ring", name="x_sb")
         sx_sb = ring.tile([P, 4096], BF16, tag="ring", name="sx_sb")
-        for g in range(4):
+        for k0, k1 in ((0, 512), (512, 1024), (1024, 2048)):
             for dst, src in ((sx_sb, state_x), (x_sb, x)):
                 nc.sync.dma_start(
-                    out=dst[:, 1024 * g : 1024 * (g + 1)].rearrange("p (r k) -> p r k", r=2),
-                    in_=src.rearrange("(r p) k -> p r k", p=P)[:, :, 512 * g : 512 * (g + 1)],
+                    out=dst[:, 2 * k0 : 2 * k1].rearrange("p (r k) -> p r k", r=2),
+                    in_=src.rearrange("(r p) k -> p r k", p=P)[:, :, k0:k1],
                 )
-        for row, src in ((0, time_decay), (32, time_first)):
-            nc.sync.dma_start(out=vec_rows[row : row + TILES, :], in_=src.rearrange("(j d) -> j d", j=TILES))
+            if k0 == 0:
+                for row, src in ((0, time_decay), (32, time_first)):
+                    nc.sync.dma_start(out=vec_rows[row : row + TILES, :], in_=src.rearrange("(j d) -> j d", j=TILES))
+
+        def row_start(g, r):
+            return 1024 * g + 512 * r if g < 2 else 2048 + 1024 * r + 512 * (g - 2)
+
         load_w(0, 0)
         load_w(1, 0)
         for i in range(3):
@@ -121,31 +126,25 @@ def tile_rwkv_timemix_for_quant_pa_kernel(
         xg = grp.tile([P, 8192], BF16, tag="grp", name="xg", align_bytes=64)
         sw = sx_sb[:].bitcast(F32)
 
-        def regroup_key(g, pln):
-            out = xg[:, 1024 * g : 1024 * (g + 1)].rearrange("p (n t) -> p n t", t=4)
-            in_ = pln[:].rearrange("p (t n) -> p n t", t=4)
-            if g < 3:
+        def regroup_x(v, g):
+            o0 = 4096 * v + 1024 * g
+            out = xg[:, o0 : o0 + 1024].rearrange("p (n t) -> p n t", t=4)
+            in_ = mixed[(v, g)][:].rearrange("p (t n) -> p n t", t=4)
+            if g == 3:
+                nc.vector.tensor_copy(out=out, in_=in_)
+            elif v == 0:
                 nc.gpsimd.tensor_scalar(out=out, in0=in_, scalar1=1.0, scalar2=0.0, op0=ALU.mult, op1=ALU.add)
             else:
-                nc.vector.tensor_copy(out=out, in_=in_)
-
-        def add_value(g):
-            o0 = 4096 + 1024 * g
-            nc.vector.tensor_tensor(
-                out=xg[:, o0 : o0 + 1024].rearrange("p (n u e) -> p n u e", u=2, e=2),
-                in0=scaled[g][:].rearrange("p (u e n) -> p n u e", u=2, e=2),
-                in1=state_x_t[g][:].rearrange("p (u n e) -> p n u e", u=2, e=2),
-                op=ALU.add,
-            )
+                nc.scalar.copy(out=out, in_=in_)
 
         state_x_t = {}
-        scaled = {}
+        mixed = {}
 
         def turn_state_x(g):
             sb = tp.tile([P, 512], F32, tag="tp", name="sb")
             for u in range(2):
                 for r in range(2):
-                    src = 512 * g + 256 * r
+                    src = row_start(g, r) // 2
                     col = 256 * u + 128 * r
                     nc.tensor.transpose(sb[:, col : col + 128], sw[:, src + u : src + 256 : 2], ident[:])
             sxs = ep.tile([P, 1024], BF16, tag=("ndd", "xf0")[g % 2], name="sxs")
@@ -155,13 +154,13 @@ def tile_rwkv_timemix_for_quant_pa_kernel(
         turn_state_x(0)
         for g in range(4):
             sxs = state_x_t[g]
-            pln = hp.tile([P, 1024], BF16, tag="p2", name="pln")
-            scaled[g] = hp.tile([P, 1024], F32, tag="t1", name="scaled")
+            for v in range(2):
+                mixed[(v, g)] = hp.tile([P, 1024], BF16, tag=("p2", "t1")[v], name="mixed")
             for u in range(2):
                 dxb = acc.tile([P, 512], F32, tag="kv"[u], name="dxb")
                 for e in range(2):
                     for r in range(2):
-                        base = 1024 * g + 512 * r
+                        base = row_start(g, r)
                         col = 256 * e + 128 * r
                         xs = x_sb[:, base : base + 512].rearrange("p (w t) -> p w t", t=4)[:, :, 2 * u + e]
                         ss = sx_sb[:, base : base + 512].rearrange("p (w t) -> p w t", t=4)[:, :, 2 * u + e]
@@ -169,33 +168,28 @@ def tile_rwkv_timemix_for_quant_pa_kernel(
                         nc.tensor.matmul(out=dxb[:, col : col + 128], lhsT=ss, rhs=nidentb[:], start=False, stop=True)
                 if u == 1 and g < 3:
                     turn_state_x(g + 1)
-                for e in range(2):
-                    t = 2 * u + e
-                    i = 4 * g + t
-                    nc.vector.scalar_tensor_tensor(
-                        out=pln[:, 256 * t : 256 * (t + 1)],
-                        in0=dxb[:, 256 * e : 256 * (e + 1)],
-                        scalar=mkf[:, i : i + 1],
-                        in1=sxs[:, 512 * u : 512 * (u + 1)].rearrange("p (n e) -> p n e", e=2)[:, :, e],
-                        op0=ALU.mult,
-                        op1=ALU.add,
-                    )
-                for e in range(2):
-                    t = 2 * u + e
-                    i = 16 + 4 * g + t
-                    nc.scalar.activation(
-                        out=scaled[g][:, 256 * t : 256 * (t + 1)],
-                        in_=dxb[:, 256 * e : 256 * (e + 1)],
-                        func=ACT.Copy,
-                        scale=mkf[:, i : i + 1],
-                    )
-            regroup_key(g, pln)
+                for v in range(2):
+                    for e in range(2):
+                        t = 2 * u + e
+                        i = 16 * v + 4 * g + t
+                        nc.vector.scalar_tensor_tensor(
+                            out=mixed[(v, g)][:, 256 * t : 256 * (t + 1)],
+                            in0=dxb[:, 256 * e : 256 * (e + 1)],
+                            scalar=mkf[:, i : i + 1],
+                            in1=sxs[:, 512 * u : 512 * (u + 1)].rearrange("p (n e) -> p n e", e=2)[:, :, e],
+                            op0=ALU.mult,
+                            op1=ALU.add,
+                        )
             if g == 0:
                 nc.gpsimd.tensor_scalar(
                     out=vec_rows[0:32, :], in0=vec_rows[0:32, :], scalar1=TD_MAX, scalar2=0.0, op0=ALU.min, op1=ALU.add
                 )
-            if 0 < g < 3:
-                add_value(g - 1)
+            regroup_x(0, g)
+            if g > 0:
+                regroup_x(1, g - 1)
+            if g == 1:
+                nc.scalar.activation(out=vec_rows_f[0:32, :], in_=vec_rows[0:32, :], func=ACT.Exp)
+                nc.scalar.copy(out=vec_rows_f[32:64, :], in_=vec_rows[32:64, :])
         load_w(1, 1)
 
         xcodes = const.tile([P, 2048], U32, name="xcodes", align_bytes=64)
@@ -265,16 +259,19 @@ def tile_rwkv_timemix_for_quant_pa_kernel(
 
         rows_ps = {}
 
-        def spread_rows(j):
-            first = acc.tile([P, NT], F32, tag="v", name="first")
+        def spread_first(j, pool, tag):
+            first = pool.tile([P, NT], F32, tag=tag, name="first")
             nc.tensor.matmul(
                 out=first[:], lhsT=identb[:, 32 + j : 33 + j].to_broadcast([P, P]), rhs=vec_rows[:], start=True, stop=True
             )
+            rows_ps[j] = [first]
+
+        def spread_delta(j):
             delta = acc.tile([P, NT], F32, tag="v", name="delta")
             nc.tensor.matmul(
                 out=delta[:], lhsT=sel[:, j : j + 1].to_broadcast([P, P]), rhs=vec_rows_f[:], start=True, stop=True
             )
-            rows_ps[j] = (first, delta)
+            rows_ps[j].append(delta)
 
         two = "p (h d) -> p h d"
 
@@ -296,10 +293,10 @@ def tile_rwkv_timemix_for_quant_pa_kernel(
             nq = [ep.tile([P, NT], F32, tag="nq", name="nq") for r in range(2)]
             for r in range(2):
                 nc.vector.tensor_tensor(
-                    out=nq[r][:], in0=per_row_tile(states[(j, 0)], r), in1=k_ps[r][:], op=ALU.subtract
+                    out=nq[r][:], in0=per_row_tile(states[(j, 0)], r), in1=first[:], op=ALU.subtract
                 )
             for r in range(2):
-                nc.vector.tensor_tensor(out=ndd[r][:, 0:NT], in0=nq[r][:], in1=first[:], op=ALU.subtract)
+                nc.vector.tensor_tensor(out=ndd[r][:, 0:NT], in0=nq[r][:], in1=k_ps[r][:], op=ALU.subtract)
             for r in range(2):
                 nc.vector.tensor_tensor(out=ndd[r][:, NT : 2 * NT], in0=ndd[r][:, 0:NT], in1=delta[:], op=ALU.add)
             for r in range(2):
@@ -374,17 +371,14 @@ def tile_rwkv_timemix_for_quant_pa_kernel(
         load_w(0, 2)
         quantise_x(0)
         quantise_w(gt_k, wq_k, (0,))
-        add_value(2)
+        regroup_x(1, 3)
         quantise_w(gt_k, wq_k, (1,))
-        nc.scalar.activation(out=vec_rows_f[0:32, :], in_=vec_rows[0:32, :], func=ACT.Exp)
-        nc.scalar.copy(out=vec_rows_f[32:64, :], in_=vec_rows[32:64, :])
-        regroup_w(1, 0, gt_v, range(3))
+        spread_first(0, acc, "v")
+        spread_delta(0)
         k_ps = new_ps(0)
         project(0, wq_k, k_ps)
-        spread_rows(0)
-        add_value(3)
         quantise_x(1)
-        regroup_w(1, 0, gt_v, range(3, 8))
+        regroup_w(1, 0, gt_v, range(8))
         xf1, xf2 = exponents(0, k_ps)
         for i in range(3):
             load_state(1, i)
@@ -412,6 +406,7 @@ def tile_rwkv_timemix_for_quant_pa_kernel(
             if not last:
                 wq_k, wq_v = new_codes(), new_codes()
                 quantise_w(gt_k, wq_k)
+                spread_first(j + 1, tp, "tp")
                 k_ps = new_ps(0)
                 project(0, wq_k, k_ps)
             t2 = []
@@ -423,7 +418,7 @@ def tile_rwkv_timemix_for_quant_pa_kernel(
                 for r in range(2):
                     numerator_halves(j, r, t1[r], t2[r])
             else:
-                spread_rows(j + 1)
+                spread_delta(j + 1)
                 regroup_w(1, j + 1, gt_v, range(4, 8))
                 xf1, xf2 = exponents(j + 1, k_ps)
                 if j == 0:

@@ -18,6 +18,7 @@ D = 2048
 NT = 512
 TILES = D // NT
 FLOPS = 2 * 2 * ROWS * E * D
+SHARED = (TILES - 1, 1)
 TD_MAX = 69.0
 
 
@@ -78,14 +79,9 @@ def tile_rwkv_timemix_for_quant_pa_kernel(
 
         warm_in = const.tile([P, 1], F32, name="warm_in")
         warm_out = const.tile([P, 1], F32, name="warm_out")
+        mix_rows = const.tile([P, 512], BF16, name="mix_rows")
+        nc.vector.memset(mix_rows[:], 0.0)
         nc.vector.memset(warm_in[:], 0.0)
-        mkb = const.tile([P, 32], BF16, name="mkb")
-        with nc.allow_non_contiguous_dma(reason="mix coefficients, four neighbouring k to a partition"):
-            for v, src in enumerate((time_mix_k, time_mix_v)):
-                nc.scalar.dma_start(
-                    out=mkb[:, 16 * v : 16 * (v + 1)].rearrange("p (g t) -> p g t", t=4),
-                    in_=src.rearrange("o (g p t) -> p (o g) t", g=4, p=P, t=4),
-                )
         nc.scalar.activation(out=warm_out[:], in_=warm_in[:], func=ACT.Exp)
         vec_rows = const.tile([P, NT], BF16, name="vec_rows")
         nc.vector.memset(vec_rows[:], 0.0)
@@ -100,6 +96,8 @@ def tile_rwkv_timemix_for_quant_pa_kernel(
                     in_=src.rearrange("(r p) k -> p r k", p=P)[:, :, k0:k1],
                 )
             if k0 == 0:
+                for v, src in enumerate((time_mix_k, time_mix_v)):
+                    nc.sync.dma_start(out=mix_rows[4 * v : 4 * v + 4, :], in_=src.rearrange("o (g k) -> (o g) k", g=4))
                 for row, src in ((0, time_decay), (32, time_first)):
                     nc.sync.dma_start(out=vec_rows[row : row + TILES, :], in_=src.rearrange("(j d) -> j d", j=TILES))
 
@@ -121,7 +119,6 @@ def tile_rwkv_timemix_for_quant_pa_kernel(
         sel = const.tile([P, TILES], F32, name="sel")
         nc.gpsimd.tensor_tensor(out=sel[:], in0=ident[:, 32 : 32 + TILES], in1=ident[:, 0:TILES], op=ALU.subtract)
         mkf = const.tile([P, 32], F32, name="mkf")
-        nc.vector.tensor_copy(out=mkf[:], in_=mkb[:])
 
         xg = grp.tile([P, 8192], BF16, tag="grp", name="xg", align_bytes=64)
         sw = sx_sb[:].bitcast(F32)
@@ -130,7 +127,7 @@ def tile_rwkv_timemix_for_quant_pa_kernel(
             o0 = 4096 * v + 1024 * g
             out = xg[:, o0 : o0 + 1024].rearrange("p (n t) -> p n t", t=4)
             in_ = mixed[(v, g)][:].rearrange("p (t n) -> p n t", t=4)
-            if g == 3:
+            if g == 3 and v == 0:
                 nc.vector.tensor_copy(out=out, in_=in_)
             elif v == 0:
                 nc.gpsimd.tensor_scalar(out=out, in0=in_, scalar1=1.0, scalar2=0.0, op0=ALU.mult, op1=ALU.add)
@@ -151,41 +148,60 @@ def tile_rwkv_timemix_for_quant_pa_kernel(
             nc.scalar.copy(out=sxs[:].bitcast(F32), in_=sb[:])
             state_x_t[g] = sxs
 
+        warm_ps = tp.tile([P, 512], F32, tag="tp", name="warm_ps")
+        for i in range(3):
+            nc.tensor.matmul(out=warm_ps[:, 128 * i : 128 * (i + 1)], lhsT=ident[:], rhs=ident[:], start=True, stop=True)
+
+        def turn_mix_rows():
+            mix_ps = tp.tile([P, 512], BF16, tag="tp", name="mix_ps")
+            for t in range(4):
+                nc.tensor.transpose(mix_ps[:, 128 * t : 128 * (t + 1)], mix_rows[:, t:512:4], identb[:])
+            nc.vector.tensor_copy(
+                out=mkf[:].rearrange("p (m t) -> p m t", t=4),
+                in_=mix_ps[:].rearrange("p (t m) -> p m t", t=4)[:, 0:8, :],
+            )
+
         turn_state_x(0)
         for g in range(4):
             sxs = state_x_t[g]
             for v in range(2):
                 mixed[(v, g)] = hp.tile([P, 1024], BF16, tag=("p2", "t1")[v], name="mixed")
             for u in range(2):
-                dxb = acc.tile([P, 512], F32, tag="kv"[u], name="dxb")
+                if g == 0:
+                    parts = [acc.tile([P, 256], F32, tag="kv"[e], name="dxb") for e in range(2)]
+                    dx = [parts[0][:], parts[1][:]]
+                else:
+                    dxb = acc.tile([P, 512], F32, tag="kv"[u], name="dxb")
+                    dx = [dxb[:, 256 * e : 256 * (e + 1)] for e in range(2)]
                 for e in range(2):
                     for r in range(2):
                         base = row_start(g, r)
-                        col = 256 * e + 128 * r
+                        cols = slice(128 * r, 128 * (r + 1))
                         xs = x_sb[:, base : base + 512].rearrange("p (w t) -> p w t", t=4)[:, :, 2 * u + e]
                         ss = sx_sb[:, base : base + 512].rearrange("p (w t) -> p w t", t=4)[:, :, 2 * u + e]
-                        nc.tensor.matmul(out=dxb[:, col : col + 128], lhsT=xs, rhs=identb[:], start=True, stop=False)
-                        nc.tensor.matmul(out=dxb[:, col : col + 128], lhsT=ss, rhs=nidentb[:], start=False, stop=True)
+                        nc.tensor.matmul(out=dx[e][:, cols], lhsT=xs, rhs=identb[:], start=True, stop=False)
+                        nc.tensor.matmul(out=dx[e][:, cols], lhsT=ss, rhs=nidentb[:], start=False, stop=True)
+                    if g == u == e == 0:
+                        turn_mix_rows()
                 if u == 1 and g < 3:
                     turn_state_x(g + 1)
-                for v in range(2):
-                    for e in range(2):
-                        t = 2 * u + e
-                        i = 16 * v + 4 * g + t
-                        nc.vector.scalar_tensor_tensor(
-                            out=mixed[(v, g)][:, 256 * t : 256 * (t + 1)],
-                            in0=dxb[:, 256 * e : 256 * (e + 1)],
-                            scalar=mkf[:, i : i + 1],
-                            in1=sxs[:, 512 * u : 512 * (u + 1)].rearrange("p (n e) -> p n e", e=2)[:, :, e],
-                            op0=ALU.mult,
-                            op1=ALU.add,
-                        )
+                for e, v in ((0, 0), (0, 1), (1, 0), (1, 1)):
+                    t = 2 * u + e
+                    i = 16 * v + 4 * g + t
+                    nc.vector.scalar_tensor_tensor(
+                        out=mixed[(v, g)][:, 256 * t : 256 * (t + 1)],
+                        in0=dx[e],
+                        scalar=mkf[:, i : i + 1],
+                        in1=sxs[:, 512 * u : 512 * (u + 1)].rearrange("p (n e) -> p n e", e=2)[:, :, e],
+                        op0=ALU.mult,
+                        op1=ALU.add,
+                    )
             if g == 0:
                 nc.gpsimd.tensor_scalar(
                     out=vec_rows[0:32, :], in0=vec_rows[0:32, :], scalar1=TD_MAX, scalar2=0.0, op0=ALU.min, op1=ALU.add
                 )
             regroup_x(0, g)
-            if g > 0:
+            if 0 < g < 3:
                 regroup_x(1, g - 1)
             if g == 1:
                 nc.scalar.activation(out=vec_rows_f[0:32, :], in_=vec_rows[0:32, :], func=ACT.Exp)
@@ -284,17 +300,20 @@ def tile_rwkv_timemix_for_quant_pa_kernel(
         def twice(ap):
             return ap.unsqueeze(1).to_broadcast([P, 2, NT])
 
-        def exponents(j, k_ps):
-            first, delta = rows_ps[j]
+        def less_first(j):
+            nq = [ep.tile([P, NT], F32, tag="nq", name="nq") for r in range(2)]
+            for r in range(2):
+                nc.vector.tensor_tensor(
+                    out=nq[r][:], in0=per_row_tile(states[(j, 0)], r), in1=rows_ps[j][0][:], op=ALU.subtract
+                )
+            return nq
+
+        def exponents(j, nq, k_ps):
+            delta = rows_ps[j][1]
             ndd = [ep.tile([P, 1024], F32, tag="ndd", name="ndd") for r in range(2)]
             xf1 = [ep.tile([P, 1024], F32, tag="xf0", name="xf1") for r in range(2)]
             xf2 = [ep.tile([P, 1024], F32, tag="xf1", name="xf2") for r in range(2)]
             p2 = [hp.tile([P, NT], F32, tag="p2", name="p2") for r in range(2)]
-            nq = [ep.tile([P, NT], F32, tag="nq", name="nq") for r in range(2)]
-            for r in range(2):
-                nc.vector.tensor_tensor(
-                    out=nq[r][:], in0=per_row_tile(states[(j, 0)], r), in1=first[:], op=ALU.subtract
-                )
             for r in range(2):
                 nc.vector.tensor_tensor(out=ndd[r][:, 0:NT], in0=nq[r][:], in1=k_ps[r][:], op=ALU.subtract)
             for r in range(2):
@@ -302,7 +321,12 @@ def tile_rwkv_timemix_for_quant_pa_kernel(
             for r in range(2):
                 nc.scalar.activation(out=xf1[r][:], in_=ndd[r][:], func=ACT.Exp)
             for r in range(2):
-                nc.scalar.activation(out=xf2[r][:], in_=ndd[r][:], func=ACT.Exp, scale=-1.0)
+                if (j, r) == SHARED:
+                    nc.scalar.activation(out=xf2[r][:, 0:NT], in_=ndd[r][:, 0:NT], func=ACT.Exp, scale=-1.0)
+                    nc.scalar.activation(out=xf2[r][:, NT:], in_=ndd[r][:, NT:], func=ACT.Relu)
+                    nc.scalar.activation(out=xf2[r][:, NT:], in_=xf2[r][:, NT:], func=ACT.Exp, scale=-1.0)
+                else:
+                    nc.scalar.activation(out=xf2[r][:], in_=ndd[r][:], func=ACT.Exp, scale=-1.0)
             for r in range(2):
                 nc.vector.scalar_tensor_tensor(
                     out=p2[r][:], in0=ndd[r][:, NT : 2 * NT], scalar=0.0, in1=k_ps[r][:], op0=ALU.max, op1=ALU.add
@@ -310,28 +334,18 @@ def tile_rwkv_timemix_for_quant_pa_kernel(
                 store(out_4, j, r, p2[r][:])
             return xf1, xf2
 
-        def state_terms(j, xf1):
-            a_t, b_t = states[(j, 1)], states[(j, 2)]
-            t1 = [hp.tile([P, 1024], F32, tag="t1", name="t1") for r in range(2)]
-            for r in range(2):
-                nc.vector.scalar_tensor_tensor(
-                    out=t1[r][:].rearrange(two, h=2),
-                    in0=xf1[r][:].rearrange(two, h=2),
-                    scalar=1.0,
-                    in1=twice(per_row_tile(a_t, r)),
-                    op0=ALU.min,
-                    op1=ALU.mult,
-                )
-            for r in range(2):
-                nc.vector.scalar_tensor_tensor(
-                    out=xf1[r][:].rearrange(two, h=2),
-                    in0=xf1[r][:].rearrange(two, h=2),
-                    scalar=1.0,
-                    in1=twice(per_row_tile(b_t, r)),
-                    op0=ALU.min,
-                    op1=ALU.mult,
-                )
-            return t1
+        def state_term(j, i, xf1, r, out):
+            nc.vector.scalar_tensor_tensor(
+                out=out[:].rearrange(two, h=2),
+                in0=xf1[r][:].rearrange(two, h=2),
+                scalar=1.0,
+                in1=twice(per_row_tile(states[(j, i)], r)),
+                op0=ALU.min,
+                op1=ALU.mult,
+            )
+
+        def new_t1():
+            return [hp.tile([P, 1024], F32, tag="t1", name="t1") for r in range(2)]
 
         def value_term(j, v_ps, xf2, r):
             t2 = ep.tile([P, 1024], F32, tag="t2", name="t2")
@@ -345,14 +359,21 @@ def tile_rwkv_timemix_for_quant_pa_kernel(
             )
             return t2
 
-        def denominators(j, xf1, xf2):
-            for r in range(2):
-                b = hp.tile([P, 1024], F32, tag="t1", name="b")
-                nc.vector.scalar_tensor_tensor(
-                    out=b[:], in0=xf2[r][:], scalar=1.0, in1=xf1[r][:], op0=ALU.min, op1=ALU.add
-                )
-                store(out_1, j, r, b[:, 0:NT])
-                store(out_3, j, r, b[:, NT : 2 * NT])
+        def denominator(j, r, xf1, xf2):
+            b = hp.tile([P, 1024], F32, tag="t1", name="b")
+            own = NT if (j, r) == SHARED else 2 * NT
+            if own == NT:
+                nc.gpsimd.tensor_tensor(out=b[:, NT:], in0=xf2[r][:, NT:], in1=xf1[r][:, NT:], op=ALU.add)
+                store(out_3, j, r, b[:, NT:])
+            return b, own
+
+        def finish_denominator(j, r, xf1, xf2, b, own):
+            nc.vector.scalar_tensor_tensor(
+                out=b[:, 0:own], in0=xf2[r][:, 0:own], scalar=1.0, in1=xf1[r][:, 0:own], op0=ALU.min, op1=ALU.add
+            )
+            store(out_1, j, r, b[:, 0:NT])
+            if own > NT:
+                store(out_3, j, r, b[:, NT:])
 
         def numerator(j, r, t1, t2):
             nc.gpsimd.tensor_tensor(out=t2[:], in0=t1[:], in1=t2[:], op=ALU.add)
@@ -368,6 +389,7 @@ def tile_rwkv_timemix_for_quant_pa_kernel(
         gt_k, gt_v = new_gt(), new_gt()
         wq_k, wq_v = new_codes(), new_codes()
         regroup_w(0, 0, gt_k, range(8))
+        regroup_x(1, 2)
         load_w(0, 2)
         quantise_x(0)
         quantise_w(gt_k, wq_k, (0,))
@@ -377,9 +399,10 @@ def tile_rwkv_timemix_for_quant_pa_kernel(
         spread_delta(0)
         k_ps = new_ps(0)
         project(0, wq_k, k_ps)
+        nq = less_first(0)
         quantise_x(1)
         regroup_w(1, 0, gt_v, range(8))
-        xf1, xf2 = exponents(0, k_ps)
+        xf1, xf2 = exponents(0, nq, k_ps)
         for i in range(3):
             load_state(1, i)
         load_w(1, 2)
@@ -390,36 +413,46 @@ def tile_rwkv_timemix_for_quant_pa_kernel(
             if not last:
                 gt_k = new_gt()
                 regroup_w(0, j + 1, gt_k, range(3), "tkk")
-            t1 = state_terms(j, xf1)
+            t1 = new_t1()
             v_ps = new_ps(1)
+            if last:
+                project(1, wq_v, v_ps)
+                state_term(j, 1, xf1, 0, t1[0])
+                state_term(j, 2, xf1, 0, xf1[0])
+                state_term(j, 1, xf1, 1, t1[1])
+                finish_denominator(j, 0, xf1, xf2, *denominator(j, 0, xf1, xf2))
+                state_term(j, 2, xf1, 1, xf1[1])
+                rest = denominator(j, 1, xf1, xf2)
+                t2 = [value_term(j, v_ps, xf2, r) for r in range(2)]
+                finish_denominator(j, 1, xf1, xf2, *rest)
+                for r in range(2):
+                    numerator_halves(j, r, t1[r], t2[r])
+                break
+            for i in (1, 2):
+                for r in range(2):
+                    state_term(j, i, xf1, r, (t1[r], xf1[r])[i - 1])
             project(1, wq_v, v_ps)
-            if not last:
-                regroup_w(0, j + 1, gt_k, range(3, 8))
-                gt_v = new_gt()
-                regroup_w(1, j + 1, gt_v, range(4))
-            denominators(j, xf1, xf2)
+            regroup_w(0, j + 1, gt_k, range(3, 8))
+            gt_v = new_gt()
+            regroup_w(1, j + 1, gt_v, range(4))
+            for r in range(2):
+                finish_denominator(j, r, xf1, xf2, *denominator(j, r, xf1, xf2))
             if j == 0:
                 load_w(0, 3)
             if j + 2 < TILES:
                 for i in range(3):
                     load_state(j + 2, i)
-            if not last:
-                wq_k, wq_v = new_codes(), new_codes()
-                quantise_w(gt_k, wq_k)
-                spread_first(j + 1, tp, "tp")
-                k_ps = new_ps(0)
-                project(0, wq_k, k_ps)
+            wq_k, wq_v = new_codes(), new_codes()
+            quantise_w(gt_k, wq_k)
+            spread_first(j + 1, tp, "tp")
+            k_ps = new_ps(0)
+            project(0, wq_k, k_ps)
             t2 = []
             for r in range(2):
                 t2.append(value_term(j, v_ps, xf2, r))
-                if not last:
-                    numerator(j, r, t1[r], t2[r])
-            if last:
-                for r in range(2):
-                    numerator_halves(j, r, t1[r], t2[r])
-            else:
-                spread_delta(j + 1)
-                regroup_w(1, j + 1, gt_v, range(4, 8))
-                xf1, xf2 = exponents(j + 1, k_ps)
-                if j == 0:
-                    load_w(1, 3)
+                numerator(j, r, t1[r], t2[r])
+            spread_delta(j + 1)
+            regroup_w(1, j + 1, gt_v, range(4, 8))
+            xf1, xf2 = exponents(j + 1, less_first(j + 1), k_ps)
+            if j == 0:
+                load_w(1, 3)

@@ -19,6 +19,7 @@ NT = 512
 TILES = D // NT
 FLOPS = 2 * 2 * ROWS * E * D
 SHARED = (TILES - 1, 1)
+EARLY = (1,)
 TD_MAX = 69.0
 
 
@@ -48,6 +49,7 @@ def tile_rwkv_timemix_for_quant_pa_kernel(
         grp = ctx.enter_context(tc.tile_pool(name="grp", bufs=3))
         cod = ctx.enter_context(tc.tile_pool(name="cod", bufs=2))
         st = ctx.enter_context(tc.tile_pool(name="st", bufs=2))
+        stp = ctx.enter_context(tc.tile_pool(name="stp", bufs=3))
         ep = ctx.enter_context(tc.tile_pool(name="ep", bufs=2))
         hp = ctx.enter_context(tc.tile_pool(name="hp", bufs=4))
         tp = ctx.enter_context(tc.psum_pool(name="tp", bufs=4))
@@ -70,7 +72,7 @@ def tile_rwkv_timemix_for_quant_pa_kernel(
 
         def load_state(j, i):
             src = (state_p, state_A, state_B)[i]
-            t = st.tile([P, 1024], BF16, tag="st%d" % i, name="st_t")
+            t = (stp if i == 0 else st).tile([P, 1024], BF16, tag="st%d" % i, name="st_t")
             nc.sync.dma_start(
                 out=t[:].rearrange("p (r d) -> p r d", r=2),
                 in_=src.rearrange("(r p) d -> p r d", p=P)[:, :, NT * j : NT * (j + 1)],
@@ -108,6 +110,8 @@ def tile_rwkv_timemix_for_quant_pa_kernel(
         load_w(1, 0)
         for i in range(3):
             load_state(0, i)
+        for j in EARLY:
+            load_state(j, 0)
         load_w(0, 1)
 
         ident = const.tile([P, P], F32, name="ident")
@@ -282,6 +286,21 @@ def tile_rwkv_timemix_for_quant_pa_kernel(
             )
             rows_ps[j] = [first]
 
+        early = {}
+
+        def early_difference(j):
+            spread_first(j, tp, "tp")
+            first = const.tile([P, NT], BF16, name="first%d" % j)
+            nc.scalar.copy(out=first[:], in_=rows_ps[j][0][:])
+            diff = ep.tile([P, 1024], F32, tag="diff", name="diff")
+            nc.gpsimd.tensor_tensor(
+                out=diff[:].rearrange("p (h d) -> p h d", h=2),
+                in0=states[(j, 0)][:].rearrange("p (h d) -> p h d", h=2),
+                in1=first[:].unsqueeze(1).to_broadcast([P, 2, NT]),
+                op=ALU.subtract,
+            )
+            early[j] = [diff[:, 0:NT], diff[:, NT:]]
+
         def spread_delta(j):
             delta = acc.tile([P, NT], F32, tag="v", name="delta")
             nc.tensor.matmul(
@@ -301,12 +320,14 @@ def tile_rwkv_timemix_for_quant_pa_kernel(
             return ap.unsqueeze(1).to_broadcast([P, 2, NT])
 
         def less_first(j):
+            if j in EARLY:
+                return early[j]
             nq = [ep.tile([P, NT], F32, tag="nq", name="nq") for r in range(2)]
             for r in range(2):
                 nc.vector.tensor_tensor(
                     out=nq[r][:], in0=per_row_tile(states[(j, 0)], r), in1=rows_ps[j][0][:], op=ALU.subtract
                 )
-            return nq
+            return [nq[0][:], nq[1][:]]
 
         def exponents(j, nq, k_ps):
             delta = rows_ps[j][1]
@@ -315,7 +336,7 @@ def tile_rwkv_timemix_for_quant_pa_kernel(
             xf2 = [ep.tile([P, 1024], F32, tag="xf1", name="xf2") for r in range(2)]
             p2 = [hp.tile([P, NT], F32, tag="p2", name="p2") for r in range(2)]
             for r in range(2):
-                nc.vector.tensor_tensor(out=ndd[r][:, 0:NT], in0=nq[r][:], in1=k_ps[r][:], op=ALU.subtract)
+                nc.vector.tensor_tensor(out=ndd[r][:, 0:NT], in0=nq[r], in1=k_ps[r][:], op=ALU.subtract)
             for r in range(2):
                 nc.vector.tensor_tensor(out=ndd[r][:, NT : 2 * NT], in0=ndd[r][:, 0:NT], in1=delta[:], op=ALU.add)
             for r in range(2):
@@ -383,8 +404,14 @@ def tile_rwkv_timemix_for_quant_pa_kernel(
         def numerator_halves(j, r, t1, t2):
             for h, dst in enumerate((out_0, out_2)):
                 cols = slice(NT * h, NT * (h + 1))
-                nc.vector.tensor_tensor(out=t2[:, cols], in0=t1[:, cols], in1=t2[:, cols], op=ALU.add)
-                store(dst, j, r, t2[:, cols])
+                if r == 0 or h == 0:
+                    nc.vector.tensor_tensor(out=t2[:, cols], in0=t1[:, cols], in1=t2[:, cols], op=ALU.add)
+                    store(dst, j, r, t2[:, cols])
+                    continue
+                for c0 in (0, 256):
+                    c = slice(NT * h + c0, NT * h + c0 + 256)
+                    nc.vector.tensor_tensor(out=t2[:, c], in0=t1[:, c], in1=t2[:, c], op=ALU.add)
+                    nc.scalar.dma_start(out=dst[P * r : P * (r + 1), NT * j + c0 : NT * j + c0 + 256], in_=t2[:, c])
 
         gt_k, gt_v = new_gt(), new_gt()
         wq_k, wq_v = new_codes(), new_codes()
@@ -401,10 +428,13 @@ def tile_rwkv_timemix_for_quant_pa_kernel(
         project(0, wq_k, k_ps)
         nq = less_first(0)
         quantise_x(1)
+        for j in EARLY:
+            early_difference(j)
         regroup_w(1, 0, gt_v, range(8))
         xf1, xf2 = exponents(0, nq, k_ps)
         for i in range(3):
-            load_state(1, i)
+            if i or 1 not in EARLY:
+                load_state(1, i)
         load_w(1, 2)
 
         for j in range(TILES):
@@ -412,7 +442,7 @@ def tile_rwkv_timemix_for_quant_pa_kernel(
             quantise_w(gt_v, wq_v)
             if not last:
                 gt_k = new_gt()
-                regroup_w(0, j + 1, gt_k, range(3), "tkk")
+                regroup_w(0, j + 1, gt_k, range(4), "ttkk")
             t1 = new_t1()
             v_ps = new_ps(1)
             if last:
@@ -432,19 +462,24 @@ def tile_rwkv_timemix_for_quant_pa_kernel(
                 for r in range(2):
                     state_term(j, i, xf1, r, (t1[r], xf1[r])[i - 1])
             project(1, wq_v, v_ps)
-            regroup_w(0, j + 1, gt_k, range(3, 8))
+            regroup_w(0, j + 1, gt_k, range(4, 8))
             gt_v = new_gt()
-            regroup_w(1, j + 1, gt_v, range(4))
+            regroup_w(1, j + 1, gt_v, range(3))
+            wq_k, wq_v = new_codes(), wq_v
             for r in range(2):
                 finish_denominator(j, r, xf1, xf2, *denominator(j, r, xf1, xf2))
+                if r == 0:
+                    quantise_w(gt_k, wq_k, (0,))
             if j == 0:
                 load_w(0, 3)
             if j + 2 < TILES:
                 for i in range(3):
-                    load_state(j + 2, i)
-            wq_k, wq_v = new_codes(), new_codes()
-            quantise_w(gt_k, wq_k)
-            spread_first(j + 1, tp, "tp")
+                    if i or j + 2 not in EARLY:
+                        load_state(j + 2, i)
+            quantise_w(gt_k, wq_k, (1,))
+            wq_v = new_codes()
+            if j + 1 not in EARLY:
+                spread_first(j + 1, tp, "tp")
             k_ps = new_ps(0)
             project(0, wq_k, k_ps)
             t2 = []
@@ -452,7 +487,7 @@ def tile_rwkv_timemix_for_quant_pa_kernel(
                 t2.append(value_term(j, v_ps, xf2, r))
                 numerator(j, r, t1[r], t2[r])
             spread_delta(j + 1)
-            regroup_w(1, j + 1, gt_v, range(4, 8))
+            regroup_w(1, j + 1, gt_v, range(3, 8))
             xf1, xf2 = exponents(j + 1, less_first(j + 1), k_ps)
             if j == 0:
                 load_w(1, 3)

@@ -64,10 +64,11 @@ def tile_rwkv_timemix_for_quant_pa_kernel(
             for h in range(2):
                 wr = ring.tile([P, 4096], BF16, tag="ring", name="wr")
                 row0 = NT * j + 256 * h
-                nc.sync.dma_start(
-                    out=wr[:].rearrange("p (c k) -> p c k", c=2),
-                    in_=weights[v][row0 : row0 + 256, :].rearrange("(c p) k -> p c k", p=P),
-                )
+                for c in range(2):
+                    nc.sync.dma_start(
+                        out=wr[:, 2048 * c : 2048 * (c + 1)],
+                        in_=weights[v][row0 + P * c : row0 + P * (c + 1), :],
+                    )
                 raw_w[(v, j, h)] = wr
 
         def load_state(j, i):

@@ -109,11 +109,12 @@ def tile_rwkv_timemix_for_quant_pa_kernel(
 
         load_w(0, 0)
         load_w(1, 0)
-        for i in range(3):
-            load_state(0, i)
+        load_state(0, 0)
         for j in EARLY:
             load_state(j, 0)
         load_w(0, 1)
+        load_state(0, 1)
+        load_state(0, 2)
 
         ident = const.tile([P, P], F32, name="ident")
         make_identity(nc, ident[:])
@@ -487,8 +488,10 @@ def tile_rwkv_timemix_for_quant_pa_kernel(
             for r in range(2):
                 t2.append(value_term(j, v_ps, xf2, r))
                 numerator(j, r, t1[r], t2[r])
+                if r == 0:
+                    nq = less_first(j + 1)
             spread_delta(j + 1)
             regroup_w(1, j + 1, gt_v, range(3, 8))
-            xf1, xf2 = exponents(j + 1, less_first(j + 1), k_ps)
+            xf1, xf2 = exponents(j + 1, nq, k_ps)
             if j == 0:
                 load_w(1, 3)

from contextlib import ExitStack

import concourse.mybir as mybir
from concourse.masks import make_identity

F32 = mybir.dt.float32
BF16 = mybir.dt.bfloat16
U32 = mybir.dt.uint32
U8 = mybir.dt.uint8
FP8X4 = mybir.dt.float8_e4m3fn_x4
ALU = mybir.AluOpType
ACT = mybir.ActivationFunctionType

P = 128
ROWS = 256
E = 2048
D = 2048
NT = 512
TILES = D // NT
FLOPS = 2 * 2 * ROWS * E * D
SHARED = (TILES - 1, 1)
EARLY = (1,)
TD_MAX = 69.0


def tile_rwkv_timemix_for_quant_pa_kernel(
    tc,
    x,
    state_A,
    state_B,
    state_p,
    state_x,
    time_decay,
    time_first,
    time_mix_k,
    time_mix_v,
    W_key,
    W_value,
    out_0,
    out_1,
    out_2,
    out_3,
    out_4,
):
    nc = tc.nc
    with ExitStack() as ctx:
        const = ctx.enter_context(tc.tile_pool(name="const", bufs=1))
        ring = ctx.enter_context(tc.tile_pool(name="ring", bufs=8))
        grp = ctx.enter_context(tc.tile_pool(name="grp", bufs=3))
        cod = ctx.enter_context(tc.tile_pool(name="cod", bufs=2))
        st = ctx.enter_context(tc.tile_pool(name="st", bufs=2))
        stp = ctx.enter_context(tc.tile_pool(name="stp", bufs=3))
        ep = ctx.enter_context(tc.tile_pool(name="ep", bufs=2))
        hp = ctx.enter_context(tc.tile_pool(name="hp", bufs=4))
        tp = ctx.enter_context(tc.psum_pool(name="tp", bufs=4))
        acc = ctx.enter_context(tc.psum_pool(name="acc", bufs=2))
        ctx.enter_context(tc.manual_schedule())

        weights = (W_key, W_value)
        raw_w = {}
        states = {}

        def load_w(v, j):
            for h in range(2):
                wr = ring.tile([P, 4096], BF16, tag="ring", name="wr")
                row0 = NT * j + 256 * h
                for c in range(2):
                    nc.sync.dma_start(
                        out=wr[:, 2048 * c : 2048 * (c + 1)],
                        in_=weights[v][row0 + P * c : row0 + P * (c + 1), :],
                    )
                raw_w[(v, j, h)] = wr

        def load_state(j, i):
            src = (state_p, state_A, state_B)[i]
            t = (stp if i == 0 else st).tile([P, 1024], BF16, tag="st%d" % i, name="st_t")
            nc.sync.dma_start(
                out=t[:].rearrange("p (r d) -> p r d", r=2),
                in_=src.rearrange("(r p) d -> p r d", p=P)[:, :, NT * j : NT * (j + 1)],
            )
            states[(j, i)] = t

        warm_in = const.tile([P, 1], F32, name="warm_in")
        warm_out = const.tile([P, 1], F32, name="warm_out")
        mix_rows = const.tile([P, 512], BF16, name="mix_rows")
        nc.vector.memset(mix_rows[:], 0.0)
        nc.vector.memset(warm_in[:], 0.0)
        nc.scalar.activation(out=warm_out[:], in_=warm_in[:], func=ACT.Exp)
        vec_rows = const.tile([P, NT], BF16, name="vec_rows")
        nc.vector.memset(vec_rows[:], 0.0)
        vec_rows_f = const.tile([P, NT], F32, name="vec_rows_f")
        nc.vector.memset(vec_rows_f[:], 0.0)
        x_sb = ring.tile([P, 4096], BF16, tag="ring", name="x_sb")
        sx_sb = ring.tile([P, 4096], BF16, tag="ring", name="sx_sb")
        for k0, k1 in ((0, 512), (512, 1024), (1024, 2048)):
            for dst, src in ((sx_sb, state_x), (x_sb, x)):
                nc.sync.dma_start(
                    out=dst[:, 2 * k0 : 2 * k1].rearrange("p (r k) -> p r k", r=2),
                    in_=src.rearrange("(r p) k -> p r k", p=P)[:, :, k0:k1],
                )
            if k0 == 0:
                for v, src in enumerate((time_mix_k, time_mix_v)):
                    nc.sync.dma_start(out=mix_rows[4 * v : 4 * v + 4, :], in_=src.rearrange("o (g k) -> (o g) k", g=4))
                for row, src in ((0, time_decay), (32, time_first)):
                    nc.sync.dma_start(out=vec_rows[row : row + TILES, :], in_=src.rearrange("(j d) -> j d", j=TILES))

        def row_start(g, r):
            return 1024 * g + 512 * r if g < 2 else 2048 + 1024 * r + 512 * (g - 2)

        load_w(0, 0)
        load_w(1, 0)
        load_state(0, 0)
        for j in EARLY:
            load_state(j, 0)
        load_w(0, 1)
        load_state(0, 1)
        load_state(0, 2)

        ident = const.tile([P, P], F32, name="ident")
        make_identity(nc, ident[:])
        identb = const.tile([P, P], BF16, name="identb")
        make_identity(nc, identb[:])
        nidentb = const.tile([P, P], BF16, name="nidentb")
        nc.gpsimd.tensor_scalar(out=nidentb[:], in0=identb[:], scalar1=-1.0, scalar2=0.0, op0=ALU.mult, op1=ALU.add)
        sel = const.tile([P, TILES], F32, name="sel")
        nc.gpsimd.tensor_tensor(out=sel[:], in0=ident[:, 32 : 32 + TILES], in1=ident[:, 0:TILES], op=ALU.subtract)
        mkf = const.tile([P, 32], F32, name="mkf")

        xg = grp.tile([P, 8192], BF16, tag="grp", name="xg", align_bytes=64)
        sw = sx_sb[:].bitcast(F32)

        def regroup_x(v, g):
            o0 = 4096 * v + 1024 * g
            out = xg[:, o0 : o0 + 1024].rearrange("p (n t) -> p n t", t=4)
            in_ = mixed[(v, g)][:].rearrange("p (t n) -> p n t", t=4)
            if g == 3 and v == 0:
                nc.vector.tensor_copy(out=out, in_=in_)
            elif v == 0:
                nc.gpsimd.tensor_scalar(out=out, in0=in_, scalar1=1.0, scalar2=0.0, op0=ALU.mult, op1=ALU.add)
            else:
                nc.scalar.copy(out=out, in_=in_)

        state_x_t = {}
        mixed = {}

        def turn_state_x(g):
            sb = tp.tile([P, 512], F32, tag="tp", name="sb")
            for u in range(2):
                for r in range(2):
                    src = row_start(g, r) // 2
                    col = 256 * u + 128 * r
                    nc.tensor.transpose(sb[:, col : col + 128], sw[:, src + u : src + 256 : 2], ident[:])
            sxs = ep.tile([P, 1024], BF16, tag=("ndd", "xf0")[g % 2], name="sxs")
            nc.scalar.copy(out=sxs[:].bitcast(F32), in_=sb[:])
            state_x_t[g] = sxs

        warm_ps = tp.tile([P, 512], F32, tag="tp", name="warm_ps")
        for i in range(3):
            nc.tensor.matmul(out=warm_ps[:, 128 * i : 128 * (i + 1)], lhsT=ident[:], rhs=ident[:], start=True, stop=True)

        def turn_mix_rows():
            mix_ps = tp.tile([P, 512], BF16, tag="tp", name="mix_ps")
            for t in range(4):
                nc.tensor.transpose(mix_ps[:, 128 * t : 128 * (t + 1)], mix_rows[:, t:512:4], identb[:])
            nc.vector.tensor_copy(
                out=mkf[:].rearrange("p (m t) -> p m t", t=4),
                in_=mix_ps[:].rearrange("p (t m) -> p m t", t=4)[:, 0:8, :],
            )

        turn_state_x(0)
        for g in range(4):
            sxs = state_x_t[g]
            for v in range(2):
                mixed[(v, g)] = hp.tile([P, 1024], BF16, tag=("p2", "t1")[v], name="mixed")
            for u in range(2):
                if g == 0:
                    parts = [acc.tile([P, 256], F32, tag="kv"[e], name="dxb") for e in range(2)]
                    dx = [parts[0][:], parts[1][:]]
                else:
                    dxb = acc.tile([P, 512], F32, tag="kv"[u], name="dxb")
                    dx = [dxb[:, 256 * e : 256 * (e + 1)] for e in range(2)]
                for e in range(2):
                    for r in range(2):
                        base = row_start(g, r)
                        cols = slice(128 * r, 128 * (r + 1))
                        xs = x_sb[:, base : base + 512].rearrange("p (w t) -> p w t", t=4)[:, :, 2 * u + e]
                        ss = sx_sb[:, base : base + 512].rearrange("p (w t) -> p w t", t=4)[:, :, 2 * u + e]
                        nc.tensor.matmul(out=dx[e][:, cols], lhsT=xs, rhs=identb[:], start=True, stop=False)
                        nc.tensor.matmul(out=dx[e][:, cols], lhsT=ss, rhs=nidentb[:], start=False, stop=True)
                    if g == u == e == 0:
                        turn_mix_rows()
                if u == 1 and g < 3:
                    turn_state_x(g + 1)
                for e, v in ((0, 0), (0, 1), (1, 0), (1, 1)):
                    t = 2 * u + e
                    i = 16 * v + 4 * g + t
                    nc.vector.scalar_tensor_tensor(
                        out=mixed[(v, g)][:, 256 * t : 256 * (t + 1)],
                        in0=dx[e],
                        scalar=mkf[:, i : i + 1],
                        in1=sxs[:, 512 * u : 512 * (u + 1)].rearrange("p (n e) -> p n e", e=2)[:, :, e],
                        op0=ALU.mult,
                        op1=ALU.add,
                    )
            if g == 0:
                nc.gpsimd.tensor_scalar(
                    out=vec_rows[0:32, :], in0=vec_rows[0:32, :], scalar1=TD_MAX, scalar2=0.0, op0=ALU.min, op1=ALU.add
                )
            regroup_x(0, g)
            if 0 < g < 3:
                regroup_x(1, g - 1)
            if g == 1:
                nc.scalar.activation(out=vec_rows_f[0:32, :], in_=vec_rows[0:32, :], func=ACT.Exp)
                nc.scalar.copy(out=vec_rows_f[32:64, :], in_=vec_rows[32:64, :])
        load_w(1, 1)

        xcodes = const.tile([P, 2048], U32, name="xcodes", align_bytes=64)
        xscl = const.tile([P, 2048], U8, name="xscl", align_bytes=64)

        def quantise_x(v):
            nc.vector.quantize_mx(
                out=xcodes[:, 1024 * v : 1024 * (v + 1)].bitcast(FP8X4),
                scales=xscl[:, 1024 * v : 1024 * (v + 1)],
                in_=xg[:, 4096 * v : 4096 * (v + 1)],
            )

        def new_gt():
            return grp.tile([P, 8192], BF16, tag="grp", name="gt", align_bytes=64)

        def regroup_w(v, j, gt, banks, tags=()):
            gw = gt[:].bitcast(F32).rearrange("p (g d u) -> p g d u", g=4, d=NT, u=2)
            for i, b in enumerate(banks):
                hb, c = b // 4, b % 4
                wf = raw_w[(v, j, c // 2)][:].bitcast(F32)
                base = 1024 * (c % 2)
                if i < len(tags) and tags[i] == "k":
                    bank = acc.tile([P, 512], F32, tag="k", name="bank")
                else:
                    bank = tp.tile([P, 512], F32, tag="tp", name="bank")
                for gi in range(2):
                    for u in range(2):
                        src = base + 256 * (2 * hb + gi)
                        col = 128 * (2 * gi + u)
                        nc.tensor.transpose(bank[:, col : col + 128], wf[:, src + u : src + 256 : 2], ident[:])
                nc.scalar.copy(
                    out=gw[:, 2 * hb : 2 * hb + 2, 128 * c : 128 * (c + 1), :],
                    in_=bank[:].rearrange("p (g u d) -> p g d u", g=2, u=2, d=128),
                )

        def new_codes():
            codes = cod.tile([P, 2048], U32, tag="codes", name="codes", align_bytes=64)
            scl = cod.tile([P, 2048], U8, tag="scl", name="scl", align_bytes=64)
            return codes, scl

        def quantise_w(gt, wq, halves=(0, 1)):
            codes, scl = wq
            for hb in halves:
                nc.vector.quantize_mx(
                    out=codes[:, 1024 * hb : 1024 * (hb + 1)].bitcast(FP8X4),
                    scales=scl[:, 1024 * hb : 1024 * (hb + 1)],
                    in_=gt[:, 4096 * hb : 4096 * (hb + 1)],
                )

        def new_ps(v):
            return [acc.tile([P, NT], F32, tag="kv"[v], name="ps") for r in range(2)]

        def project(v, wq, ps, groups=range(4)):
            codes, scl = wq
            for g in groups:
                for r in range(2):
                    c0 = 1024 * v + 256 * g + 128 * r
                    nc.tensor.matmul_mx(
                        out=ps[r][:],
                        lhsT=xcodes[:, c0 : c0 + 128].bitcast(FP8X4),
                        lhsT_scale=xscl[:, c0 : c0 + 128],
                        rhs=codes[:, NT * g : NT * (g + 1)].bitcast(FP8X4),
                        rhs_scale=scl[:, NT * g : NT * (g + 1)],
                        start=(g == 0),
                        stop=(g == 3),
                    )

        rows_ps = {}

        def spread_first(j, pool, tag):
            first = pool.tile([P, NT], F32, tag=tag, name="first")
            nc.tensor.matmul(
                out=first[:], lhsT=identb[:, 32 + j : 33 + j].to_broadcast([P, P]), rhs=vec_rows[:], start=True, stop=True
            )
            rows_ps[j] = [first]

        early = {}

        def early_difference(j):
            spread_first(j, tp, "tp")
            first = const.tile([P, NT], BF16, name="first%d" % j)
            nc.scalar.copy(out=first[:], in_=rows_ps[j][0][:])
            diff = ep.tile([P, 1024], F32, tag="diff", name="diff")
            nc.gpsimd.tensor_tensor(
                out=diff[:].rearrange("p (h d) -> p h d", h=2),
                in0=states[(j, 0)][:].rearrange("p (h d) -> p h d", h=2),
                in1=first[:].unsqueeze(1).to_broadcast([P, 2, NT]),
                op=ALU.subtract,
            )
            early[j] = [diff[:, 0:NT], diff[:, NT:]]

        def spread_delta(j):
            delta = acc.tile([P, NT], F32, tag="v", name="delta")
            nc.tensor.matmul(
                out=delta[:], lhsT=sel[:, j : j + 1].to_broadcast([P, P]), rhs=vec_rows_f[:], start=True, stop=True
            )
            rows_ps[j].append(delta)

        two = "p (h d) -> p h d"

        def store(dst, j, r, src):
            nc.sync.dma_start(out=dst[P * r : P * (r + 1), NT * j : NT * (j + 1)], in_=src)

        def per_row_tile(t, r):
            return t[:, NT * r : NT * (r + 1)]

        def twice(ap):
            return ap.unsqueeze(1).to_broadcast([P, 2, NT])

        def less_first(j):
            if j in EARLY:
                return early[j]
            nq = [ep.tile([P, NT], F32, tag="nq", name="nq") for r in range(2)]
            for r in range(2):
                nc.vector.tensor_tensor(
                    out=nq[r][:], in0=per_row_tile(states[(j, 0)], r), in1=rows_ps[j][0][:], op=ALU.subtract
                )
            return [nq[0][:], nq[1][:]]

        def exponents(j, nq, k_ps):
            delta = rows_ps[j][1]
            ndd = [ep.tile([P, 1024], F32, tag="ndd", name="ndd") for r in range(2)]
            xf1 = [ep.tile([P, 1024], F32, tag="xf0", name="xf1") for r in range(2)]
            xf2 = [ep.tile([P, 1024], F32, tag="xf1", name="xf2") for r in range(2)]
            p2 = [hp.tile([P, NT], F32, tag="p2", name="p2") for r in range(2)]
            for r in range(2):
                nc.vector.tensor_tensor(out=ndd[r][:, 0:NT], in0=nq[r], in1=k_ps[r][:], op=ALU.subtract)
            for r in range(2):
                nc.vector.tensor_tensor(out=ndd[r][:, NT : 2 * NT], in0=ndd[r][:, 0:NT], in1=delta[:], op=ALU.add)
            for r in range(2):
                nc.scalar.activation(out=xf1[r][:], in_=ndd[r][:], func=ACT.Exp)
            for r in range(2):
                if (j, r) == SHARED:
                    nc.scalar.activation(out=xf2[r][:, 0:NT], in_=ndd[r][:, 0:NT], func=ACT.Exp, scale=-1.0)
                    nc.scalar.activation(out=xf2[r][:, NT:], in_=ndd[r][:, NT:], func=ACT.Relu)
                    nc.scalar.activation(out=xf2[r][:, NT:], in_=xf2[r][:, NT:], func=ACT.Exp, scale=-1.0)
                else:
                    nc.scalar.activation(out=xf2[r][:], in_=ndd[r][:], func=ACT.Exp, scale=-1.0)
            for r in range(2):
                nc.vector.scalar_tensor_tensor(
                    out=p2[r][:], in0=ndd[r][:, NT : 2 * NT], scalar=0.0, in1=k_ps[r][:], op0=ALU.max, op1=ALU.add
                )
                store(out_4, j, r, p2[r][:])
            return xf1, xf2

        def state_term(j, i, xf1, r, out):
            nc.vector.scalar_tensor_tensor(
                out=out[:].rearrange(two, h=2),
                in0=xf1[r][:].rearrange(two, h=2),
                scalar=1.0,
                in1=twice(per_row_tile(states[(j, i)], r)),
                op0=ALU.min,
                op1=ALU.mult,
            )

        def new_t1():
            return [hp.tile([P, 1024], F32, tag="t1", name="t1") for r in range(2)]

        def value_term(j, v_ps, xf2, r):
            t2 = ep.tile([P, 1024], F32, tag="t2", name="t2")
            nc.vector.scalar_tensor_tensor(
                out=t2[:].rearrange(two, h=2),
                in0=xf2[r][:].rearrange(two, h=2),
                scalar=1.0,
                in1=twice(v_ps[r][:]),
                op0=ALU.min,
                op1=ALU.mult,
            )
            return t2

        def denominator(j, r, xf1, xf2):
            b = hp.tile([P, 1024], F32, tag="t1", name="b")
            own = NT if (j, r) == SHARED else 2 * NT
            if own == NT:
                nc.gpsimd.tensor_tensor(out=b[:, NT:], in0=xf2[r][:, NT:], in1=xf1[r][:, NT:], op=ALU.add)
                store(out_3, j, r, b[:, NT:])
            return b, own

        def finish_denominator(j, r, xf1, xf2, b, own):
            nc.vector.scalar_tensor_tensor(
                out=b[:, 0:own], in0=xf2[r][:, 0:own], scalar=1.0, in1=xf1[r][:, 0:own], op0=ALU.min, op1=ALU.add
            )
            store(out_1, j, r, b[:, 0:NT])
            if own > NT:
                store(out_3, j, r, b[:, NT:])

        def numerator(j, r, t1, t2):
            nc.gpsimd.tensor_tensor(out=t2[:], in0=t1[:], in1=t2[:], op=ALU.add)
            store(out_0, j, r, t2[:, 0:NT])
            store(out_2, j, r, t2[:, NT : 2 * NT])

        def numerator_halves(j, r, t1, t2):
            for h, dst in enumerate((out_0, out_2)):
                cols = slice(NT * h, NT * (h + 1))
                if r == 0 or h == 0:
                    nc.vector.tensor_tensor(out=t2[:, cols], in0=t1[:, cols], in1=t2[:, cols], op=ALU.add)
                    store(dst, j, r, t2[:, cols])
                    continue
                for c0 in (0, 256):
                    c = slice(NT * h + c0, NT * h + c0 + 256)
                    nc.vector.tensor_tensor(out=t2[:, c], in0=t1[:, c], in1=t2[:, c], op=ALU.add)
                    nc.scalar.dma_start(out=dst[P * r : P * (r + 1), NT * j + c0 : NT * j + c0 + 256], in_=t2[:, c])

        gt_k, gt_v = new_gt(), new_gt()
        wq_k, wq_v = new_codes(), new_codes()
        regroup_w(0, 0, gt_k, range(8))
        regroup_x(1, 2)
        load_w(0, 2)
        quantise_x(0)
        quantise_w(gt_k, wq_k, (0,))
        regroup_x(1, 3)
        quantise_w(gt_k, wq_k, (1,))
        spread_first(0, acc, "v")
        spread_delta(0)
        k_ps = new_ps(0)
        project(0, wq_k, k_ps)
        nq = less_first(0)
        quantise_x(1)
        for j in EARLY:
            early_difference(j)
        regroup_w(1, 0, gt_v, range(8))
        xf1, xf2 = exponents(0, nq, k_ps)
        for i in range(3):
            if i or 1 not in EARLY:
                load_state(1, i)
        load_w(1, 2)

        for j in range(TILES):
            last = j + 1 == TILES
            quantise_w(gt_v, wq_v)
            if not last:
                gt_k = new_gt()
                regroup_w(0, j + 1, gt_k, range(4), "ttkk")
            t1 = new_t1()
            v_ps = new_ps(1)
            if last:
                project(1, wq_v, v_ps)
                state_term(j, 1, xf1, 0, t1[0])
                state_term(j, 2, xf1, 0, xf1[0])
                state_term(j, 1, xf1, 1, t1[1])
                finish_denominator(j, 0, xf1, xf2, *denominator(j, 0, xf1, xf2))
                state_term(j, 2, xf1, 1, xf1[1])
                rest = denominator(j, 1, xf1, xf2)
                t2 = [value_term(j, v_ps, xf2, r) for r in range(2)]
                finish_denominator(j, 1, xf1, xf2, *rest)
                for r in range(2):
                    numerator_halves(j, r, t1[r], t2[r])
                break
            for i in (1, 2):
                for r in range(2):
                    state_term(j, i, xf1, r, (t1[r], xf1[r])[i - 1])
            project(1, wq_v, v_ps)
            regroup_w(0, j + 1, gt_k, range(4, 8))
            gt_v = new_gt()
            regroup_w(1, j + 1, gt_v, range(3))
            wq_k, wq_v = new_codes(), wq_v
            for r in range(2):
                finish_denominator(j, r, xf1, xf2, *denominator(j, r, xf1, xf2))
                if r == 0:
                    quantise_w(gt_k, wq_k, (0,))
            if j == 0:
                load_w(0, 3)
            if j + 2 < TILES:
                for i in range(3):
                    if i or j + 2 not in EARLY:
                        load_state(j + 2, i)
            quantise_w(gt_k, wq_k, (1,))
            wq_v = new_codes()
            if j + 1 not in EARLY:
                spread_first(j + 1, tp, "tp")
            k_ps = new_ps(0)
            project(0, wq_k, k_ps)
            t2 = []
            for r in range(2):
                t2.append(value_term(j, v_ps, xf2, r))
                numerator(j, r, t1[r], t2[r])
                if r == 0:
                    nq = less_first(j + 1)
            spread_delta(j + 1)
            regroup_w(1, j + 1, gt_v, range(3, 8))
            xf1, xf2 = exponents(j + 1, nq, k_ps)
            if j == 0:
                load_w(1, 3)
